import numpy as np
import ml_dtypes


def mxq(x, axis, fmt="e4m3"):
    dtype, down = {"e4m3": (ml_dtypes.float8_e4m3fn, 7), "e5m2": (ml_dtypes.float8_e5m2, 14)}[fmt]
    v = np.moveaxis(np.asarray(x, np.float32).astype(ml_dtypes.bfloat16).astype(np.float64), axis, -1)
    blocks = v.reshape(v.shape[:-1] + (-1, 32))
    amax = np.abs(blocks).max(-1, keepdims=True)
    byte = np.maximum(np.where(amax > 0, np.frexp(amax)[1] - 1 + 127, 0) - down, 1)
    scale = np.exp2(byte - 127.0)
    codes = (blocks / scale).astype(np.float32).astype(dtype).astype(np.float64)
    return np.moveaxis((codes * scale).reshape(v.shape), -1, axis)


WIDE = False


def mx_kscale(k):
    if not WIDE:
        return np.ones(k)
    levels = np.array([10, -10, 5, -5, 0])
    if k % 512:
        return np.exp2(np.random.permutation(np.resize(levels, k // 32))).repeat(32)
    a = np.empty((k // 512, 16))
    for p in range(k // 512):
        a[p, :8] = np.random.permutation(np.resize(levels, 8))
        for g in range(8):
            far = levels[np.abs(levels - a[p, g]) >= 10]
            a[p, g + 8] = far[np.random.randint(len(far))]
    return np.exp2(a.ravel()).repeat(32)


BF16 = ml_dtypes.bfloat16


def bf(x):
    return np.asarray(x, np.float32).astype(BF16)


def f64(x):
    return np.asarray(x).astype(np.float64)


B, I, H, AH, AI, G = 512, 1024, 1024, 128, 128, 4
EPS = 1e-5


def sigmoid(v):
    return 1.0 / (1.0 + np.exp(-v))


def ln(v, w, b):
    mu = v.mean(-1, keepdims=True)
    var = ((v - mu) ** 2).mean(-1, keepdims=True)
    return (v - mu) / np.sqrt(var + EPS) * w + b


def setup_inputs():
    n = np.random.standard_normal
    s, t = mx_kscale(I), mx_kscale(H)
    return {
        "x": bf(n((B, I)) * s),
        "hx": bf(n((B, H)) * t),
        "cx": bf(n((B, H))),
        "zw": bf(1.0 + 0.5 * n((B, 2 * G, AI))),
        "zb": bf(0.7 * n((B, 2 * G, AI))),
        "w_ih": bf(n((G * H, I)) / np.sqrt(I) / s),
        "w_hh": bf(n((G * H, H)) / np.sqrt(H) / t),
        "b_ih": bf(0.2 * n(G * H)),
        "b_hh": bf(0.2 * n(G * H)),
        "norm_alpha_w": bf(n((2 * G, H, AI)) / np.sqrt(AI)),
        "bias_beta_w": bf(0.7 * n((2 * G, H, AI)) / np.sqrt(AI)),
        "ln_i_w": bf(1.0 + 0.1 * n(G * H)),
        "ln_i_b": bf(0.2 * n(G * H)),
        "ln_h_w": bf(1.0 + 0.1 * n(G * H)),
        "ln_h_b": bf(0.2 * n(G * H)),
        "ln_c_w": bf(1.0 + 0.1 * n(H)),
        "ln_c_b": bf(0.2 * n(H)),
    }


def reference(x, hx, cx, zw, zb, w_ih, w_hh, b_ih, b_hh, norm_alpha_w, bias_beta_w, ln_i_w, ln_i_b, ln_h_w, ln_h_b, ln_c_w, ln_c_b):
    alpha = (f64(zw).transpose(1, 0, 2) @ f64(norm_alpha_w).transpose(0, 2, 1)).transpose(1, 0, 2)
    beta = (f64(zb).transpose(1, 0, 2) @ f64(bias_beta_w).transpose(0, 2, 1)).transpose(1, 0, 2)
    xh = (mxq(f64(x), 1, "e4m3") @ mxq(f64(w_ih), 1, "e4m3").T).reshape(-1, G, H)
    hh = (mxq(f64(hx), 1, "e4m3") @ mxq(f64(w_hh), 1, "e4m3").T).reshape(-1, G, H)
    in_g = (xh * alpha[:, :G] + f64(b_ih).reshape(G, H) + beta[:, :G]).reshape(-1, G * H)
    hid_g = (hh * alpha[:, G:] + f64(b_hh).reshape(G, H) + beta[:, G:]).reshape(-1, G * H)
    gates = ln(in_g, f64(ln_i_w), f64(ln_i_b)) + ln(hid_g, f64(ln_h_w), f64(ln_h_b))
    i, j, f, o = np.split(gates, G, axis=1)
    cy = ln(sigmoid(f) * f64(cx) + sigmoid(i) * np.tanh(j), f64(ln_c_w), f64(ln_c_b))
    hy = sigmoid(o) * np.tanh(cy)
    return hy, cy

@@ -1,0 +1,603 @@
+from contextlib import ExitStack
+
+import concourse.mybir as mybir
+from concourse.masks import make_identity
+
+F32 = mybir.dt.float32
+BF16 = mybir.dt.bfloat16
+U32 = mybir.dt.uint32
+U8 = mybir.dt.uint8
+FP8X4 = mybir.dt.float8_e4m3fn_x4
+ALU = mybir.AluOpType
+ACT = mybir.ActivationFunctionType
+AX = mybir.AxisListType
+
+P = 128
+B = 512
+K = 1024
+H = 1024
+NBT = B // P
+NCOL = 4 * H
+CH = 512
+NCH = NCOL // CH
+NUNIT = 2 * NCH * NBT
+NHB = H // P
+EPS = 1e-5
+GATE_I = 0
+GATE_J = 1
+GATE_F = 2
+GATE_O = 3
+
+COL_B_IH = 0
+COL_LN_I_W = 32
+COL_LN_H_W = 64
+COL_LN_C_W = 96
+COL_LN_C_B = 104
+COL_LN_I_B = 128
+COL_LN_H_B = 160
+
+FLOPS = 2 * 2 * B * NCOL * K + 16 * 2 * B * H * 128
+
+
+def tile_adaptivelstmcell_pb_kernel(
+    tc, x, hx, cx, zw, zb, w_ih, w_hh, b_ih, b_hh, norm_alpha_w, bias_beta_w,
+    ln_i_w, ln_i_b, ln_h_w, ln_h_b, ln_c_w, ln_c_b, out_0, out_1,
+):
+    nc = tc.nc
+    with ExitStack() as whole:
+        whole.enter_context(tc.manual_schedule())
+        keep = whole.enter_context(tc.tile_pool(name="keep", bufs=1))
+
+        u_in = keep.tile([P, NBT * NCOL], F32, name="u_in")
+        u_hid = keep.tile([P, NBT * NCOL], F32, name="u_hid")
+        ident_f = keep.tile([P, P], F32, name="ident_f")
+        ident_b = keep.tile([P, P], BF16, name="ident_b")
+        act_words = [keep.tile([P, 2, B], U32, name="act_words%d" % h, align_bytes=64) for h in range(2)]
+        act_scales = [keep.tile([P, 2, B], U8, name="act_scales%d" % h, align_bytes=64) for h in range(2)]
+        zT = [keep.tile([P, 8, B], BF16, name="zT%d" % i) for i in range(2)]
+        b_hh_rows = keep.tile([P, CH], BF16, name="b_hh_rows")
+        vec_rows = keep.tile([P, 2, P], BF16, name="vec_rows")
+        vecT = keep.tile([P, 2 * P], BF16, name="vecT")
+        vecT_f = keep.tile([P, 2 * P], F32, name="vecT_f")
+        shiftT = keep.tile([P, 32], F32, name="shiftT")
+        neg_half = keep.tile([P, NBT], F32, name="neg_half")
+        warm = keep.tile([P, 1], F32, name="warm")
+        row_sum = keep.tile([P, 2, NBT, NCH], F32, name="row_sum")
+        row_sq = keep.tile([P, 2, NBT, NCH], F32, name="row_sq")
+        bias_sum = keep.tile([P, NCH], F32, name="bias_sum")
+        unused = keep.tile([P, H], BF16, name="unused")
+
+        def copy_on(engine, out, in_):
+            if engine == "scalar":
+                nc.scalar.copy(out=out, in_=in_)
+            else:
+                nc.vector.tensor_copy(out=out, in_=in_)
+
+        def rows_on_partitions(ap2d):
+            return ap2d.rearrange("(r p) k -> p r k", p=P)
+
+        def flat(t):
+            return t[:].rearrange("p b c -> p (b c)")
+
+        def layer_norm_scalars(name, total, total_sq, count, extra):
+            mean = keep.tile([P, NBT], F32, name="mean_" + name)
+            work = keep.tile([P, NBT], F32, name="work_" + name)
+            var = keep.tile([P, NBT], F32, name="var_" + name)
+            rstd = keep.tile([P, NBT], F32, name="rstd_" + name)
+            neg_mean = keep.tile([P, NBT], F32, name="neg_mean_" + name)
+            shift = keep.tile([P, NBT], F32, name="shift_" + name)
+            if extra is None:
+                nc.vector.tensor_scalar(out=mean[:], in0=total, scalar1=1.0 / count, scalar2=None, op0=ALU.mult)
+            else:
+                nc.vector.tensor_scalar(out=mean[:], in0=total, scalar1=extra, scalar2=1.0 / count,
+                                        op0=ALU.add, op1=ALU.mult)
+            nc.vector.tensor_tensor(out=work[:], in0=mean[:], in1=mean[:], op=ALU.mult)
+            nc.vector.tensor_scalar(out=neg_mean[:], in0=mean[:], scalar1=-1.0, scalar2=None, op0=ALU.mult)
+            nc.vector.scalar_tensor_tensor(out=var[:], in0=total_sq, scalar=1.0 / count, in1=work[:],
+                                           op0=ALU.mult, op1=ALU.subtract)
+            nc.vector.tensor_scalar(out=var[:], in0=var[:], scalar1=0.0, scalar2=EPS, op0=ALU.max, op1=ALU.add)
+            nc.gpsimd.tensor_tensor(out=rstd[:], in0=var[:], in1=neg_half[:], op=ALU.pow)
+            nc.gpsimd.tensor_tensor(out=shift[:], in0=neg_mean[:], in1=rstd[:], op=ALU.mult)
+            return (mean, rstd, shift)
+
+        def half_scalars(half):
+            total = keep.tile([P, NBT], F32, name="total%d" % half)
+            total_sq = keep.tile([P, NBT], F32, name="total_sq%d" % half)
+            nc.vector.tensor_reduce(out=total[:], in_=row_sum[:, half, :, :], axis=AX.X, op=ALU.add)
+            nc.vector.tensor_reduce(out=total_sq[:], in_=row_sq[:, half, :, :], axis=AX.X, op=ALU.add)
+            extra = None
+            if half == 0:
+                bias_total = keep.tile([P, 1], F32, name="bias_total")
+                nc.vector.tensor_reduce(out=bias_total[:], in_=bias_sum[:], axis=AX.X, op=ALU.add)
+                extra = bias_total[:]
+            return layer_norm_scalars("half%d" % half, total[:], total_sq[:], NCOL, extra)
+
+        nc.vector.memset(neg_half[:], -0.5)
+        nc.scalar.activation(out=warm[:], in_=neg_half[:, 0:1], func=ACT.Sigmoid)
+        nc.vector.memset(vec_rows[:], 0.0)
+        nc.vector.memset(b_hh_rows[:], 0.0)
+        make_identity(nc, ident_f[:])
+        make_identity(nc, ident_b[:])
+
+        with ExitStack() as stream:
+            ps_t = stream.enter_context(tc.psum_pool(name="ps_t", bufs=2))
+            ps_xh = stream.enter_context(tc.psum_pool(name="ps_xh", bufs=2))
+            ps_alpha = stream.enter_context(tc.psum_pool(name="ps_alpha", bufs=2))
+            ps_beta = stream.enter_context(tc.psum_pool(name="ps_beta", bufs=2))
+            raw_pool = stream.enter_context(tc.tile_pool(name="raw_pool", bufs=3))
+            hyper_raw_pool = stream.enter_context(tc.tile_pool(name="hyper_raw_pool", bufs=2))
+            grouped_pool = stream.enter_context(tc.tile_pool(name="grouped_pool", bufs=3))
+            mx_pool = stream.enter_context(tc.tile_pool(name="mx_pool", bufs=2))
+            hyper_pool = stream.enter_context(tc.tile_pool(name="hyper_pool", bufs=2))
+            alpha_pool = stream.enter_context(tc.tile_pool(name="alpha_pool", bufs=3))
+            bias_pool = stream.enter_context(tc.tile_pool(name="bias_pool", bufs=2))
+
+            def staged_words(i):
+                return u_hid[:, i * 2048:(i + 1) * 2048]
+
+            def staged_z(i, part):
+                first = 4096 + (2 * i + part) * 1024
+                return u_hid[:, first:first + 1024].bitcast(BF16).rearrange("p (r k) -> p r k", r=NBT)
+
+            z_rows = [rows_on_partitions(z.rearrange("b s a -> b (s a)")) for z in (zw, zb)]
+
+            def load_words(dst, src):
+                nc.sync.dma_start(out=dst.bitcast(BF16).rearrange("p (r k) -> p r k", r=4), in_=rows_on_partitions(src))
+
+            def load_z(i, part):
+                nc.sync.dma_start(out=staged_z(i, part), in_=z_rows[i][:, :, 512 * part:512 * (part + 1)])
+
+            raw = {}
+            hyper_raw = {}
+
+            def load_weights(c):
+                if c < 2 * NCH:
+                    w = w_ih if c < NCH else w_hh
+                    raw[c] = raw_pool.tile([P, 2048], F32, name="raw")
+                    load_words(raw[c][:], w[(c % NCH) * CH:(c % NCH + 1) * CH, :])
+
+            def load_hyper(s):
+                if s < 8:
+                    ra = hyper_raw_pool.tile([P, 8, P], BF16, name="raw_alpha")
+                    rb = hyper_raw_pool.tile([P, 8, P], BF16, name="raw_beta")
+                    nc.sync.dma_start(out=ra[:], in_=norm_alpha_w[s, :, :].rearrange("(r p) a -> p r a", p=P))
+                    nc.sync.dma_start(out=rb[:], in_=bias_beta_w[s, :, :].rearrange("(r p) a -> p r a", p=P))
+                    hyper_raw[s] = (ra, rb)
+
+            waiting = []
+            grouped = {}
+            w_words = {}
+            w_scales = {}
+            hyper = {}
+            bias_rows = {}
+
+            def copy_waiting():
+                for (engine, out, in_, accum_out) in waiting:
+                    if accum_out is None:
+                        copy_on(engine, out, in_)
+                    else:
+                        nc.scalar.activation(out=out, in_=in_, func=ACT.Copy, accum_out=accum_out)
+                waiting[:] = []
+
+            def new_bank(shape, dtype):
+                if len(waiting) == 2:
+                    copy_waiting()
+                return ps_t.tile(shape, dtype, name="bank")
+
+            def transpose_words(operand, src, j, engine):
+                g = j // 2
+                h = j % 2
+                if h == 0:
+                    grouped[(operand, g)] = grouped_pool.tile([P, 4 * CH], BF16, name="grouped", align_bytes=64)
+                bank = new_bank([P, 2, 2, P], F32)
+                for u in range(2):
+                    for r in range(2):
+                        first = (2 * h + r) * 512 + 256 * g
+                        nc.tensor.transpose(bank[:, u, r, :], src[:, first + u:first + 2 * P:2], ident_f[:])
+                pairs = grouped[(operand, g)][:].bitcast(F32).rearrange("p (n u) -> p n u", u=2)
+                waiting.append((engine, pairs[:, 256 * h:256 * (h + 1), :], bank[:].rearrange("p u r c -> p (r c) u"), None))
+
+            def quantise(operand, g, words, scales):
+                nc.vector.quantize_mx(out=words[:, g, :].bitcast(FP8X4), scales=scales[:, g, :],
+                                      in_=grouped[(operand, g)][:])
+
+            def transpose_z(i, part, pair, engine):
+                src = staged_z(i, part)
+                bank = new_bank([P, 4, 2, P], BF16)
+                for s in range(4):
+                    for t in range(2):
+                        nc.tensor.transpose(bank[:, s, t, :], src[:, 2 * pair + t, s * P:(s + 1) * P], ident_b[:])
+                waiting.append((engine, zT[i][:, 4 * part:4 * part + 4, 256 * pair:256 * (pair + 1)],
+                                bank[:].rearrange("p s t b -> p s (t b)"), None))
+
+            def transpose_hyper(c):
+                bank = new_bank([P, 2, 4, P], BF16)
+                for i in range(2):
+                    for r in range(4):
+                        nc.tensor.transpose(bank[:, i, r, :], hyper_raw[c // 2][i][:, (c % 2) * 4 + r, :], ident_b[:])
+                hyper[c] = hyper_pool.tile([P, 2, CH], BF16, name="hyper")
+                waiting.append(("scalar", hyper[c][:], bank[:].rearrange("p i r c -> p i (r c)"), None))
+
+            def transpose_vectors():
+                bank = new_bank([P, 2, P], BF16)
+                for i in range(2):
+                    nc.tensor.transpose(bank[:, i, :], vec_rows[:, i, :], ident_b[:])
+                nc.vector.tensor_copy(out=vecT[:], in_=bank[:].rearrange("p i c -> p (i c)"))
+                nc.vector.tensor_tensor(out=shiftT[:], in0=vecT[:, COL_LN_I_B:COL_LN_I_B + 32],
+                                        in1=vecT[:, COL_LN_H_B:COL_LN_H_B + 32], op=ALU.add)
+                nc.vector.tensor_copy(out=vecT_f[:], in_=vecT[:])
+
+            def spread_bias(c):
+                bank = new_bank([P, 4, P], BF16)
+                for m in range(4):
+                    col = COL_B_IH + 4 * c + m
+                    nc.tensor.transpose(bank[:, m, :], vecT[:, col:col + 1].to_broadcast([P, P]), ident_b[:])
+                bias_rows[c] = bias_pool.tile([P, CH], BF16, name="bias_rows")
+                waiting.append(("scalar", bias_rows[c][:], bank[:].rearrange("p m c -> p (m c)"), bias_sum[:, c:c + 1]))
+
+            load_words(staged_words(0), x)
+            load_weights(0)
+            load_z(0, 0)
+            load_z(1, 0)
+            load_hyper(0)
+            load_weights(1)
+            for (i, row, vec) in ((0, COL_B_IH, b_ih), (0, COL_LN_I_W, ln_i_w), (0, COL_LN_H_W, ln_h_w),
+                                  (0, COL_LN_C_W, ln_c_w), (0, COL_LN_C_B, ln_c_b),
+                                  (1, COL_LN_I_B - P, ln_i_b), (1, COL_LN_H_B - P, ln_h_b)):
+                nc.sync.dma_start(out=vec_rows[row:row + vec.shape[0] // P, i, :], in_=vec.rearrange("(m p) -> m p", p=P))
+            nc.sync.dma_start(out=b_hh_rows[0:NCH, :], in_=b_hh.rearrange("(c n) -> c n", c=NCH))
+            load_hyper(1)
+            load_weights(2)
+
+            def new_mx_tiles(c):
+                w_words[c] = mx_pool.tile([P, 2, CH], U32, name="w_words", align_bytes=64)
+                w_scales[c] = mx_pool.tile([P, 2, CH], U8, name="w_scales", align_bytes=64)
+
+            for j in range(4):
+                transpose_words("x", staged_words(0), j, ("scalar", "vector")[j % 2])
+            copy_waiting()
+            quantise("x", 0, act_words[0], act_scales[0])
+            new_mx_tiles(0)
+            for j in range(4):
+                transpose_words(0, raw[0][:], j, ("scalar", "vector")[j % 2])
+                if j == 1:
+                    copy_waiting()
+                    quantise("x", 1, act_words[0], act_scales[0])
+            copy_waiting()
+            quantise(0, 0, w_words[0], w_scales[0])
+            load_weights(3)
+            for i in range(2):
+                transpose_z(i, 0, 0, "scalar")
+                transpose_z(i, 0, 1, "vector")
+                copy_waiting()
+                if i == 0:
+                    quantise(0, 1, w_words[0], w_scales[0])
+            transpose_hyper(0)
+            copy_waiting()
+
+            alpha_ps = {}
+            alpha_sb = {}
+            beta_ps = {}
+
+            def where(n):
+                c = n // NBT
+                bt = n % NBT
+                half = c // NCH
+                first = bt * NCOL + (c % NCH) * CH
+                return (c, bt, half, (u_in, u_hid)[half][:, first:first + CH])
+
+            def alpha_of(n):
+                (c, bt, half, u) = where(n)
+                alpha_ps[n] = ps_alpha.tile([P, CH], F32, name="alpha_ps")
+                nc.tensor.matmul(alpha_ps[n][:], lhsT=zT[0][:, c // 2, bt * P:(bt + 1) * P], rhs=hyper[c][:, 0, :],
+                                 start=True, stop=True)
+                alpha_sb[n] = alpha_pool.tile([P, CH], F32, name="alpha_sb")
+                nc.scalar.copy(out=alpha_sb[n][:], in_=alpha_ps[n][:])
+
+            def banks_of_step(n):
+                c = n // NBT
+                r = n % NBT
+                second = "vector" if c < NCH - 1 else "scalar"
+                if n == 0:
+                    transpose_vectors()
+                    spread_bias(0)
+                    for j in range(4):
+                        transpose_words(1, raw[1][:], j, ("scalar", "vector")[j % 2])
+                    load_weights(4)
+                    load_words(staged_words(1), hx)
+                    load_z(0, 1)
+                    load_z(1, 1)
+                elif r == 0 and c + 1 < 2 * NCH:
+                    transpose_words(c + 1, raw[c + 1][:], 3, "scalar")
+                    load_weights(c + 4)
+                elif r > 0 and c + 2 < 2 * NCH:
+                    transpose_words(c + 2, raw[c + 2][:], r - 1, ("scalar", second, "scalar")[r - 1])
+                if r == 1 and c + 1 < 2 * NCH:
+                    transpose_hyper(c + 1)
+                    if c % 2 == 0:
+                        load_hyper(c // 2 + 2)
+                if r == 2 and c + 1 < NCH:
+                    spread_bias(c + 1)
+                if 3 <= c <= 6 and r in (0, 3):
+                    e = 2 * (c - 3) + r // 3
+                    if e < 4:
+                        transpose_words("hx", staged_words(1), e, ("scalar", "vector")[e % 2])
+                    else:
+                        transpose_z((e - 4) // 2, 1, e % 2, ("scalar", "vector")[e % 2])
+
+            def quantise_in_step(n):
+                c = n // NBT
+                r = n % NBT
+                if c + 1 < 2 * NCH and n > 0:
+                    if r == (1 if c == 0 else 0):
+                        new_mx_tiles(c + 1)
+                        quantise(c + 1, 0, w_words[c + 1], w_scales[c + 1])
+                    if r == 2:
+                        quantise(c + 1, 1, w_words[c + 1], w_scales[c + 1])
+                if r == 1 and c in (4, 5):
+                    quantise("hx", c - 4, act_words[1], act_scales[1])
+
+            def add_beta(n):
+                (c, bt, half, u) = where(n)
+                nc.vector.scalar_tensor_tensor(out=u, in0=u, scalar=1.0, in1=beta_ps[n][:], op0=ALU.mult, op1=ALU.add,
+                                               accum_out=row_sum[:, half, bt, c % NCH:c % NCH + 1])
+                if half == 0:
+                    nc.gpsimd.tensor_tensor(out=u, in0=u, in1=bias_rows[c][:], op=ALU.add)
+
+            def sum_squares(n):
+                (c, bt, half, u) = where(n)
+                nc.scalar.activation(out=unused[:, 0:CH], in_=u, func=ACT.Square,
+                                     accum_out=row_sq[:, half, bt, c % NCH:c % NCH + 1])
+
+            def normalise_input_half():
+                for i in range(NCH):
+                    for bt in range(NBT):
+                        cols = u_in[:, bt * NCOL + i * CH:bt * NCOL + (i + 1) * CH]
+                        nc.gpsimd.tensor_scalar(out=cols, in0=cols, scalar1=scal_in[1][:, bt:bt + 1],
+                                                scalar2=scal_in[2][:, bt:bt + 1], op0=ALU.mult, op1=ALU.add)
+
+            FIRST_HID = NCH * NBT
+            scal_in = None
+            alpha_of(0)
+            for n in range(NUNIT):
+                (c, bt, half, u) = where(n)
+                rows = slice(bt * P, (bt + 1) * P)
+                xh = ps_xh.tile([P, CH], F32, name="xh")
+                for g in range(2):
+                    nc.tensor.matmul_mx(
+                        out=xh[:],
+                        lhsT=act_words[half][:, g, rows].bitcast(FP8X4),
+                        lhsT_scale=act_scales[half][:, g, rows],
+                        rhs=w_words[c][:, g, :].bitcast(FP8X4),
+                        rhs_scale=w_scales[c][:, g, :],
+                        start=(g == 0),
+                        stop=(g == 1),
+                    )
+                copy_waiting()
+                if n + 1 < NUNIT:
+                    alpha_of(n + 1)
+                banks_of_step(n)
+                beta_ps[n] = ps_beta.tile([P, CH], F32, name="beta_ps")
+                nc.tensor.matmul(beta_ps[n][:], lhsT=zT[1][:, c // 2, rows], rhs=hyper[c][:, 1, :], start=True,
+                                 stop=(half == 0))
+                if half == 1:
+                    nc.tensor.matmul(beta_ps[n][:], lhsT=ident_b[:, c % NCH:c % NCH + 1].to_broadcast([P, P]),
+                                     rhs=b_hh_rows[:], start=False, stop=True)
+                if n >= 3:
+                    sum_squares(n - 3)
+                quantise_in_step(n)
+                nc.vector.tensor_tensor(out=u, in0=xh[:], in1=alpha_sb[n][:], op=ALU.mult)
+                if n >= 1:
+                    add_beta(n - 1)
+                if n == FIRST_HID + 2:
+                    scal_in = half_scalars(0)
+                    normalise_input_half()
+            add_beta(NUNIT - 1)
+            for n in range(NUNIT - 3, NUNIT):
+                sum_squares(n)
+            scal_hid = half_scalars(1)
+
+        with ExitStack() as tail:
+            tail_keep = tail.enter_context(tc.tile_pool(name="tail_keep", bufs=1))
+            part_pool = tail.enter_context(tc.tile_pool(name="part_pool", bufs=3))
+            gate_pool = tail.enter_context(tc.tile_pool(name="gate_pool", bufs=2))
+            ps_a = tail.enter_context(tc.psum_pool(name="ps_a", bufs=3))
+            ps_b = tail.enter_context(tc.psum_pool(name="ps_b", bufs=3))
+            ps_c = tail.enter_context(tc.psum_pool(name="ps_c", bufs=2))
+            cx_rows = tail_keep.tile([P, NBT, H], BF16, name="cx_rows")
+            nc.sync.dma_start(out=cx_rows[:], in_=rows_on_partitions(cx))
+            cellT = tail_keep.tile([P, NHB, B], F32, name="cellT")
+            outT = tail_keep.tile([P, NHB, B], F32, name="outT")
+            ln_c_w_rows = tail_keep.tile([P, H], BF16, name="ln_c_w_rows")
+            ln_c_b_rows = tail_keep.tile([P, H], BF16, name="ln_c_b_rows")
+
+            in_T = {}
+            hid_T = {}
+            hid_part = {}
+            gate = {}
+            cxT = {}
+
+            def normalise_hidden_half(hb):
+                for bt in range(NBT):
+                    cols = u_hid[:, bt * NCOL:(bt + 1) * NCOL].rearrange("p (q h) -> p q h", q=4)[:, :, hb * P:(hb + 1) * P]
+                    nc.vector.tensor_scalar(out=cols, in0=cols, scalar1=scal_hid[0][:, bt:bt + 1],
+                                            scalar2=scal_hid[1][:, bt:bt + 1], op0=ALU.subtract, op1=ALU.mult)
+
+            def columns_to_partitions(key, src, pool, store):
+                (hb, q) = key
+                store[key] = pool.tile([P, NBT, P], F32, name="turned")
+                for bt in range(NBT):
+                    first = bt * NCOL + q * H + hb * P
+                    nc.tensor.transpose(store[key][:, bt, :], src[:, first:first + P], ident_f[:])
+
+            def turn_cx(hb):
+                cxT[hb] = ps_c.tile([P, NBT, P], BF16, name="turned")
+                for bt in range(NBT):
+                    nc.tensor.transpose(cxT[hb][:, bt, :], cx_rows[:, bt, hb * P:(hb + 1) * P], ident_b[:])
+
+            def hidden_part(key):
+                (hb, q) = key
+                m = q * NHB + hb
+                if q == GATE_O:
+                    hid_part[key] = outT[:, hb, :]
+                else:
+                    t = part_pool.tile([P, B], F32, name="part")
+                    hid_part[key] = t[:]
+                nc.scalar.activation(out=hid_part[key], in_=flat(hid_T[key]), func=ACT.Identity,
+                                     scale=vecT_f[:, COL_LN_H_W + m:COL_LN_H_W + m + 1], bias=shiftT[:, m:m + 1])
+
+            def pre_activation(key):
+                (hb, q) = key
+                m = q * NHB + hb
+                if q == GATE_O:
+                    gate[key] = outT[:, hb, :]
+                else:
+                    t = gate_pool.tile([P, B], F32, name="gate%d" % q)
+                    gate[key] = t[:]
+                nc.vector.scalar_tensor_tensor(out=gate[key], in0=flat(in_T[key]),
+                                               scalar=vecT_f[:, COL_LN_I_W + m:COL_LN_I_W + m + 1], in1=hid_part[key],
+                                               op0=ALU.mult, op1=ALU.add)
+
+            def activate(key):
+                nc.scalar.activation(out=gate[key], in_=gate[key], func=(ACT.Tanh if key[1] == GATE_J else ACT.Sigmoid))
+
+            def forget_times_cx(hb):
+                nc.vector.tensor_tensor(out=gate[(hb, GATE_F)], in0=gate[(hb, GATE_F)], in1=flat(cxT[hb]), op=ALU.mult)
+
+            def new_cell(hb):
+                engine = nc.gpsimd if hb < NHB - 1 else nc.vector
+                engine.tensor_tensor(out=gate[(hb, GATE_I)], in0=gate[(hb, GATE_I)], in1=gate[(hb, GATE_J)], op=ALU.mult)
+                engine.tensor_tensor(out=cellT[:, hb, :], in0=gate[(hb, GATE_F)], in1=gate[(hb, GATE_I)], op=ALU.add)
+
+            def spread_row(col, dst):
+                bank = ps_c.tile([P, 8, P], BF16, name="turned")
+                for m in range(8):
+                    nc.tensor.transpose(bank[:, m, :], vecT[:, col + m:col + m + 1].to_broadcast([P, P]), ident_b[:])
+                nc.scalar.copy(out=dst, in_=bank[:].rearrange("p m c -> p (m c)"))
+
+            items = [(hb, q) for hb in range(NHB) for q in (GATE_F, GATE_I, GATE_J)]
+            spread_row(COL_LN_C_W, ln_c_w_rows[:])
+            spread_row(COL_LN_C_B, ln_c_b_rows[:])
+            columns_to_partitions(items[0], u_in, ps_a, in_T)
+            columns_to_partitions(items[1], u_in, ps_a, in_T)
+            normalise_hidden_half(0)
+            for t in range(-2, len(items) + 1):
+                if t + 2 < len(items):
+                    key = items[t + 2]
+                    if t + 2 >= 2:
+                        columns_to_partitions(key, u_in, ps_a, in_T)
+                    columns_to_partitions(key, u_hid, ps_b, hid_T)
+                    if key[1] == GATE_J:
+                        columns_to_partitions((key[0], GATE_O), u_hid, ps_b, hid_T)
+                        turn_cx(key[0])
+                if 0 <= t + 1 < len(items):
+                    hidden_part(items[t + 1])
+                if t >= 1:
+                    activate(items[t - 1])
+                    if items[t - 1][1] == GATE_J:
+                        new_cell(items[t - 1][0])
+                if 0 <= t < len(items):
+                    (hb, q) = items[t]
+                    if q == GATE_J:
+                        hidden_part((hb, GATE_O))
+                    pre_activation(items[t])
+                    if q == GATE_F and hb + 1 < NHB:
+                        normalise_hidden_half(hb + 1)
+                    if q == GATE_J:
+                        forget_times_cx(hb)
+
+            cell_sum = keep.tile([P, NBT, 2], F32, name="cell_sum")
+            cell_sq = keep.tile([P, NBT, 2], F32, name="cell_sq")
+            cell_mean = keep.tile([P, NBT], F32, name="cell_mean")
+            cell_msq = keep.tile([P, NBT], F32, name="cell_msq")
+            cell_var = keep.tile([P, NBT], F32, name="cell_var")
+            cell_rstd = keep.tile([P, NBT], F32, name="cell_rstd")
+            cell_rows = {}
+            out_rows = {}
+
+            def cy_of(bt):
+                return u_in[:, bt * NCOL:bt * NCOL + H]
+
+            def hy_of(bt):
+                return u_in[:, bt * NCOL + H:bt * NCOL + 2 * H]
+
+            def rows_to_partitions(bt, hf, src, pool, store):
+                store[(bt, hf)] = pool.tile([P, 4, P], F32, name="turned")
+                for i in range(4):
+                    nc.tensor.transpose(store[(bt, hf)][:, i, :], src[:, 4 * hf + i, bt * P:(bt + 1) * P], ident_f[:])
+
+            def cell_sums(bt, hf):
+                nc.scalar.activation(out=unused[:, 0:CH], in_=flat(cell_rows[(bt, hf)]), func=ACT.Copy, scale=1.0 / H,
+                                     accum_out=cell_sum[:, bt, hf:hf + 1])
+                nc.scalar.activation(out=unused[:, CH:2 * CH], in_=flat(cell_rows[(bt, hf)]), func=ACT.Square,
+                                     scale=1.0 / 32.0, accum_out=cell_sq[:, bt, hf:hf + 1])
+
+            def cell_scalars(bt, stage):
+                one = slice(bt, bt + 1)
+                if stage == 0:
+                    nc.vector.tensor_tensor(out=cell_mean[:, one], in0=cell_sum[:, bt, 0:1], in1=cell_sum[:, bt, 1:2],
+                                            op=ALU.add)
+                    nc.vector.scalar_tensor_tensor(out=cell_msq[:, one], in0=cell_sq[:, bt, 0:1], scalar=EPS,
+                                                   in1=cell_sq[:, bt, 1:2], op0=ALU.add, op1=ALU.add)
+                if stage == 1:
+                    nc.vector.scalar_tensor_tensor(out=cell_var[:, one], in0=cell_mean[:, one], scalar=cell_mean[:, one],
+                                                   in1=cell_msq[:, one], op0=ALU.mult, op1=ALU.subtract)
+                if stage == 2:
+                    nc.vector.tensor_scalar(out=cell_var[:, one], in0=cell_var[:, one], scalar1=-1.0, scalar2=EPS,
+                                            op0=ALU.mult, op1=ALU.max)
+                    nc.gpsimd.tensor_tensor(out=cell_rstd[:, one], in0=cell_var[:, one], in1=neg_half[:, one], op=ALU.pow)
+
+            def centre_and_gain(bt, hf):
+                cols = slice(hf * CH, (hf + 1) * CH)
+                nc.vector.scalar_tensor_tensor(out=cy_of(bt)[:, cols], in0=flat(cell_rows[(bt, hf)]),
+                                               scalar=cell_mean[:, bt:bt + 1], in1=ln_c_w_rows[:, cols],
+                                               op0=ALU.subtract, op1=ALU.mult)
+
+            def finish_cy(bt):
+                nc.vector.scalar_tensor_tensor(out=cy_of(bt), in0=cy_of(bt), scalar=cell_rstd[:, bt:bt + 1],
+                                               in1=ln_c_b_rows[:], op0=ALU.mult, op1=ALU.add)
+                nc.sync.dma_start(out=out_1[bt * P:(bt + 1) * P, :], in_=cy_of(bt))
+                nc.scalar.activation(out=hy_of(bt), in_=cy_of(bt), func=ACT.Tanh)
+
+            def finish_hy(bt, hf):
+                cols = slice(hf * CH, (hf + 1) * CH)
+                nc.vector.tensor_tensor(out=hy_of(bt)[:, cols], in0=hy_of(bt)[:, cols], in1=flat(out_rows[(bt, hf)]),
+                                        op=ALU.mult)
+                if hf == 1:
+                    nc.sync.dma_start(out=out_0[bt * P:(bt + 1) * P, :], in_=hy_of(bt))
+
+            def turn_out_gate(hb):
+                if hb < NHB:
+                    columns_to_partitions((hb, GATE_O), u_in, ps_c, in_T)
+
+            turn_out_gate(0)
+            turn_out_gate(1)
+            for bt in range(NBT + 1):
+                if bt < NBT:
+                    rows_to_partitions(bt, 0, cellT, ps_a, cell_rows)
+                    cell_sums(bt, 0)
+                    pre_activation((2 * bt, GATE_O))
+                if bt > 0:
+                    cell_scalars(bt - 1, 0)
+                    centre_and_gain(bt - 1, 0)
+                    cell_scalars(bt - 1, 1)
+                if bt < NBT:
+                    rows_to_partitions(bt, 1, cellT, ps_a, cell_rows)
+                    cell_sums(bt, 1)
+                    turn_out_gate(2 * bt + 2)
+                    pre_activation((2 * bt + 1, GATE_O))
+                    turn_out_gate(2 * bt + 3)
+                    activate((2 * bt, GATE_O))
+                    activate((2 * bt + 1, GATE_O))
+                if bt > 0:
+                    centre_and_gain(bt - 1, 1)
+                    cell_scalars(bt - 1, 2)
+                if bt > 1:
+                    finish_cy(bt - 2)
+            for bt in range(NBT):
+                rows_to_partitions(bt, 0, outT, ps_b, out_rows)
+                rows_to_partitions(bt, 1, outT, ps_b, out_rows)
+                finish_hy(bt, 0)
+                if bt == 0:
+                    finish_cy(NBT - 1)
+                finish_hy(bt, 1)

@@ -401,15 +401,15 @@ def tile_adaptivelstmcell_pb_kernel(
             tail_keep = tail.enter_context(tc.tile_pool(name="tail_keep", bufs=1))
             part_pool = tail.enter_context(tc.tile_pool(name="part_pool", bufs=3))
             gate_pool = tail.enter_context(tc.tile_pool(name="gate_pool", bufs=2))
-            ps_a = tail.enter_context(tc.psum_pool(name="ps_a", bufs=3))
-            ps_b = tail.enter_context(tc.psum_pool(name="ps_b", bufs=3))
+            ps_a = tail.enter_context(tc.psum_pool(name="ps_a", bufs=4))
+            ps_b = tail.enter_context(tc.psum_pool(name="ps_b", bufs=2))
             ps_c = tail.enter_context(tc.psum_pool(name="ps_c", bufs=2))
             cx_rows = tail_keep.tile([P, NBT, H], BF16, name="cx_rows")
             nc.sync.dma_start(out=cx_rows[:], in_=rows_on_partitions(cx))
-            cellT = tail_keep.tile([P, NHB, B], F32, name="cellT")
-            outT = tail_keep.tile([P, NHB, B], F32, name="outT")
             ln_c_w_rows = tail_keep.tile([P, H], BF16, name="ln_c_w_rows")
             ln_c_b_rows = tail_keep.tile([P, H], BF16, name="ln_c_b_rows")
+            cellT = tail_keep.tile([P, NHB, B], F32, name="cellT")
+            outT = tail_keep.tile([P, NHB, B], F32, name="outT")
 
             in_T = {}
             hid_T = {}
@@ -475,12 +475,13 @@ def tile_adaptivelstmcell_pb_kernel(
                     nc.tensor.transpose(bank[:, m, :], vecT[:, col + m:col + m + 1].to_broadcast([P, P]), ident_b[:])
                 nc.scalar.copy(out=dst, in_=bank[:].rearrange("p m c -> p (m c)"))
 
-            items = [(hb, q) for hb in range(NHB) for q in (GATE_F, GATE_I, GATE_J)]
+            items = [(hb, q) for hb in range(NHB) for q in (GATE_F, GATE_I, GATE_J, GATE_O)]
             spread_row(COL_LN_C_W, ln_c_w_rows[:])
             spread_row(COL_LN_C_B, ln_c_b_rows[:])
             columns_to_partitions(items[0], u_in, ps_a, in_T)
             columns_to_partitions(items[1], u_in, ps_a, in_T)
             normalise_hidden_half(0)
+            normalise_hidden_half(1)
             for t in range(-2, len(items) + 1):
                 if t + 2 < len(items):
                     key = items[t + 2]
@@ -488,23 +489,20 @@ def tile_adaptivelstmcell_pb_kernel(
                         columns_to_partitions(key, u_in, ps_a, in_T)
                     columns_to_partitions(key, u_hid, ps_b, hid_T)
                     if key[1] == GATE_J:
-                        columns_to_partitions((key[0], GATE_O), u_hid, ps_b, hid_T)
                         turn_cx(key[0])
                 if 0 <= t + 1 < len(items):
                     hidden_part(items[t + 1])
-                if t >= 1:
+                if t >= 1 and items[t - 1][1] != GATE_O:
                     activate(items[t - 1])
                     if items[t - 1][1] == GATE_J:
                         new_cell(items[t - 1][0])
                 if 0 <= t < len(items):
                     (hb, q) = items[t]
-                    if q == GATE_J:
-                        hidden_part((hb, GATE_O))
                     pre_activation(items[t])
-                    if q == GATE_F and hb + 1 < NHB:
-                        normalise_hidden_half(hb + 1)
                     if q == GATE_J:
                         forget_times_cx(hb)
+                        if hb + 2 < NHB:
+                            normalise_hidden_half(hb + 2)
 
             cell_sum = keep.tile([P, NBT, 2], F32, name="cell_sum")
             cell_sq = keep.tile([P, NBT, 2], F32, name="cell_sq")
@@ -527,16 +525,19 @@ def tile_adaptivelstmcell_pb_kernel(
                     nc.tensor.transpose(store[(bt, hf)][:, i, :], src[:, 4 * hf + i, bt * P:(bt + 1) * P], ident_f[:])
 
             def cell_sums(bt, hf):
-                nc.scalar.activation(out=unused[:, 0:CH], in_=flat(cell_rows[(bt, hf)]), func=ACT.Copy, scale=1.0 / H,
-                                     accum_out=cell_sum[:, bt, hf:hf + 1])
-                nc.scalar.activation(out=unused[:, CH:2 * CH], in_=flat(cell_rows[(bt, hf)]), func=ACT.Square,
-                                     scale=1.0 / 32.0, accum_out=cell_sq[:, bt, hf:hf + 1])
+                row = flat(cell_rows[(bt, hf)])
+                nc.scalar.activation(out=unused[:, CH:2 * CH], in_=row, func=ACT.Square, scale=1.0 / 32.0,
+                                     accum_out=cell_sq[:, bt, hf:hf + 1])
+                if bt < 2:
+                    nc.vector.tensor_reduce(out=cell_sum[:, bt, hf:hf + 1], in_=row, axis=AX.X, op=ALU.add)
+                else:
+                    nc.scalar.activation(out=unused[:, 0:CH], in_=row, func=ACT.Copy, accum_out=cell_sum[:, bt, hf:hf + 1])
 
             def cell_scalars(bt, stage):
                 one = slice(bt, bt + 1)
                 if stage == 0:
-                    nc.vector.tensor_tensor(out=cell_mean[:, one], in0=cell_sum[:, bt, 0:1], in1=cell_sum[:, bt, 1:2],
-                                            op=ALU.add)
+                    nc.vector.tensor_scalar(out=cell_mean[:, one], in0=cell_sum[:, bt, 0:1], scalar1=cell_sum[:, bt, 1:2],
+                                            scalar2=1.0 / H, op0=ALU.add, op1=ALU.mult)
                     nc.vector.scalar_tensor_tensor(out=cell_msq[:, one], in0=cell_sq[:, bt, 0:1], scalar=EPS,
                                                    in1=cell_sq[:, bt, 1:2], op0=ALU.add, op1=ALU.add)
                 if stage == 1:
@@ -566,38 +567,31 @@ def tile_adaptivelstmcell_pb_kernel(
                 if hf == 1:
                     nc.sync.dma_start(out=out_0[bt * P:(bt + 1) * P, :], in_=hy_of(bt))
 
-            def turn_out_gate(hb):
-                if hb < NHB:
-                    columns_to_partitions((hb, GATE_O), u_in, ps_c, in_T)
+            def cell_norm(bt):
+                cell_scalars(bt, 0)
+                centre_and_gain(bt, 0)
+                cell_scalars(bt, 1)
+                centre_and_gain(bt, 1)
+                cell_scalars(bt, 2)
 
-            turn_out_gate(0)
-            turn_out_gate(1)
-            for bt in range(NBT + 1):
-                if bt < NBT:
-                    rows_to_partitions(bt, 0, cellT, ps_a, cell_rows)
-                    cell_sums(bt, 0)
-                    pre_activation((2 * bt, GATE_O))
-                if bt > 0:
-                    cell_scalars(bt - 1, 0)
-                    centre_and_gain(bt - 1, 0)
-                    cell_scalars(bt - 1, 1)
-                if bt < NBT:
-                    rows_to_partitions(bt, 1, cellT, ps_a, cell_rows)
-                    cell_sums(bt, 1)
-                    turn_out_gate(2 * bt + 2)
-                    pre_activation((2 * bt + 1, GATE_O))
-                    turn_out_gate(2 * bt + 3)
-                    activate((2 * bt, GATE_O))
-                    activate((2 * bt + 1, GATE_O))
-                if bt > 0:
-                    centre_and_gain(bt - 1, 1)
-                    cell_scalars(bt - 1, 2)
-                if bt > 1:
-                    finish_cy(bt - 2)
+            banks = [ps_a] * 4 + [ps_b] * 2 + [ps_c] * 2
             for bt in range(NBT):
-                rows_to_partitions(bt, 0, outT, ps_b, out_rows)
-                rows_to_partitions(bt, 1, outT, ps_b, out_rows)
-                finish_hy(bt, 0)
-                if bt == 0:
-                    finish_cy(NBT - 1)
-                finish_hy(bt, 1)
+                for hf in range(2):
+                    rows_to_partitions(bt, hf, cellT, banks[2 * bt + hf], cell_rows)
+                    cell_sums(bt, hf)
+            cell_norm(0)
+            cell_norm(1)
+            finish_cy(0)
+            for hb in range(NHB // 2):
+                activate((hb, GATE_O))
+            cell_norm(2)
+            finish_cy(1)
+            for hb in range(NHB // 2, NHB):
+                activate((hb, GATE_O))
+            cell_norm(3)
+            finish_cy(2)
+            finish_cy(3)
+            for bt in range(NBT):
+                for hf in range(2):
+                    rows_to_partitions(bt, hf, outT, banks[2 * bt + hf], out_rows)
+                    finish_hy(bt, hf)

@@ -129,7 +129,7 @@ def tile_adaptivelstmcell_pb_kernel(
             grouped_pool = stream.enter_context(tc.tile_pool(name="grouped_pool", bufs=3))
             mx_pool = stream.enter_context(tc.tile_pool(name="mx_pool", bufs=2))
             hyper_pool = stream.enter_context(tc.tile_pool(name="hyper_pool", bufs=2))
-            alpha_pool = stream.enter_context(tc.tile_pool(name="alpha_pool", bufs=3))
+            alpha_pool = stream.enter_context(tc.tile_pool(name="alpha_pool", bufs=4))
             bias_pool = stream.enter_context(tc.tile_pool(name="bias_pool", bufs=2))
 
             def staged_words(i):
@@ -179,10 +179,15 @@ def tile_adaptivelstmcell_pb_kernel(
                         nc.scalar.activation(out=out, in_=in_, func=ACT.Copy, accum_out=accum_out)
                 waiting[:] = []
 
+            homes = [(ps_t, "bank"), (ps_xh, "xh"), (ps_alpha, "alpha_ps"), (ps_beta, "beta_ps")]
+            made = []
+
             def new_bank(shape, dtype):
-                if len(waiting) == 2:
+                if len(waiting) == 2 * len(homes):
                     copy_waiting()
-                return ps_t.tile(shape, dtype, name="bank")
+                made.append(shape)
+                (pool, tag) = homes[len(made) % len(homes)]
+                return pool.tile(shape, dtype, name=tag)
 
             def transpose_words(operand, src, j, engine):
                 g = j // 2
@@ -253,27 +258,24 @@ def tile_adaptivelstmcell_pb_kernel(
                 w_words[c] = mx_pool.tile([P, 2, CH], U32, name="w_words", align_bytes=64)
                 w_scales[c] = mx_pool.tile([P, 2, CH], U8, name="w_scales", align_bytes=64)
 
-            for j in range(4):
-                transpose_words("x", staged_words(0), j, ("scalar", "vector")[j % 2])
-            copy_waiting()
-            quantise("x", 0, act_words[0], act_scales[0])
             new_mx_tiles(0)
             for j in range(4):
+                transpose_words("x", staged_words(0), j, ("scalar", "vector")[j % 2])
+                copy_waiting()
+            for j in range(4):
                 transpose_words(0, raw[0][:], j, ("scalar", "vector")[j % 2])
-                if j == 1:
-                    copy_waiting()
-                    quantise("x", 1, act_words[0], act_scales[0])
-            copy_waiting()
-            quantise(0, 0, w_words[0], w_scales[0])
+                copy_waiting()
+                if j % 2 == 1:
+                    quantise("x", j // 2, act_words[0], act_scales[0])
             load_weights(3)
             for i in range(2):
                 transpose_z(i, 0, 0, "scalar")
                 transpose_z(i, 0, 1, "vector")
                 copy_waiting()
-                if i == 0:
-                    quantise(0, 1, w_words[0], w_scales[0])
+                quantise(0, i, w_words[0], w_scales[0])
             transpose_hyper(0)
             copy_waiting()
+            homes[:] = homes[0:1]
 
             alpha_ps = {}
             alpha_sb = {}
@@ -383,8 +385,10 @@ def tile_adaptivelstmcell_pb_kernel(
                 if half == 1:
                     nc.tensor.matmul(beta_ps[n][:], lhsT=ident_b[:, c % NCH:c % NCH + 1].to_broadcast([P, P]),
                                      rhs=b_hh_rows[:], start=False, stop=True)
-                if n >= 3:
+                if 3 <= n < FIRST_HID + 3:
                     sum_squares(n - 3)
+                if n >= FIRST_HID + 2:
+                    sum_squares(n - 2)
                 quantise_in_step(n)
                 nc.vector.tensor_tensor(out=u, in0=xh[:], in1=alpha_sb[n][:], op=ALU.mult)
                 if n >= 1:
@@ -393,7 +397,7 @@ def tile_adaptivelstmcell_pb_kernel(
                     scal_in = half_scalars(0)
                     normalise_input_half()
             add_beta(NUNIT - 1)
-            for n in range(NUNIT - 3, NUNIT):
+            for n in range(NUNIT - 2, NUNIT):
                 sum_squares(n)
             scal_hid = half_scalars(1)
 

@@ -64,7 +64,8 @@ def tile_adaptivelstmcell_pb_kernel(
         warm = keep.tile([P, 1], F32, name="warm")
         row_sum = keep.tile([P, 2, NBT, NCH], F32, name="row_sum")
         row_sq = keep.tile([P, 2, NBT, NCH], F32, name="row_sq")
-        bias_sum = keep.tile([P, NCH], F32, name="bias_sum")
+        bias_part = keep.tile([P, 1], F32, name="bias_part")
+        bias_total = keep.tile([P, 1], F32, name="bias_total")
         unused = keep.tile([P, H], BF16, name="unused")
 
         def copy_on(engine, out, in_):
@@ -79,38 +80,29 @@ def tile_adaptivelstmcell_pb_kernel(
         def flat(t):
             return t[:].rearrange("p b c -> p (b c)")
 
-        def layer_norm_scalars(name, total, total_sq, count, extra):
-            mean = keep.tile([P, NBT], F32, name="mean_" + name)
-            work = keep.tile([P, NBT], F32, name="work_" + name)
-            var = keep.tile([P, NBT], F32, name="var_" + name)
-            rstd = keep.tile([P, NBT], F32, name="rstd_" + name)
-            neg_mean = keep.tile([P, NBT], F32, name="neg_mean_" + name)
-            shift = keep.tile([P, NBT], F32, name="shift_" + name)
-            if extra is None:
-                nc.vector.tensor_scalar(out=mean[:], in0=total, scalar1=1.0 / count, scalar2=None, op0=ALU.mult)
-            else:
-                nc.vector.tensor_scalar(out=mean[:], in0=total, scalar1=extra, scalar2=1.0 / count,
-                                        op0=ALU.add, op1=ALU.mult)
-            nc.vector.tensor_tensor(out=work[:], in0=mean[:], in1=mean[:], op=ALU.mult)
-            nc.vector.tensor_scalar(out=neg_mean[:], in0=mean[:], scalar1=-1.0, scalar2=None, op0=ALU.mult)
-            nc.vector.scalar_tensor_tensor(out=var[:], in0=total_sq, scalar=1.0 / count, in1=work[:],
-                                           op0=ALU.mult, op1=ALU.subtract)
-            nc.vector.tensor_scalar(out=var[:], in0=var[:], scalar1=0.0, scalar2=EPS, op0=ALU.max, op1=ALU.add)
-            nc.gpsimd.tensor_tensor(out=rstd[:], in0=var[:], in1=neg_half[:], op=ALU.pow)
-            nc.gpsimd.tensor_tensor(out=shift[:], in0=neg_mean[:], in1=rstd[:], op=ALU.mult)
-            return (mean, rstd, shift)
-
         def half_scalars(half):
             total = keep.tile([P, NBT], F32, name="total%d" % half)
             total_sq = keep.tile([P, NBT], F32, name="total_sq%d" % half)
+            mean = keep.tile([P, NBT], F32, name="mean%d" % half)
+            mean_sq = keep.tile([P, NBT], F32, name="mean_sq%d" % half)
+            var = keep.tile([P, NBT], F32, name="var%d" % half)
+            rstd = keep.tile([P, NBT], F32, name="rstd%d" % half)
             nc.vector.tensor_reduce(out=total[:], in_=row_sum[:, half, :, :], axis=AX.X, op=ALU.add)
+            nc.vector.tensor_scalar(out=mean[:], in0=total[:], scalar1=bias_total[:] if half == 0 else 0.0, scalar2=1.0 / NCOL,
+                                    op0=ALU.add, op1=ALU.mult)
+            nc.vector.tensor_tensor(out=mean_sq[:], in0=mean[:], in1=mean[:], op=ALU.mult)
             nc.vector.tensor_reduce(out=total_sq[:], in_=row_sq[:, half, :, :], axis=AX.X, op=ALU.add)
-            extra = None
-            if half == 0:
-                bias_total = keep.tile([P, 1], F32, name="bias_total")
-                nc.vector.tensor_reduce(out=bias_total[:], in_=bias_sum[:], axis=AX.X, op=ALU.add)
-                extra = bias_total[:]
-            return layer_norm_scalars("half%d" % half, total[:], total_sq[:], NCOL, extra)
+            nc.vector.scalar_tensor_tensor(out=var[:], in0=total_sq[:], scalar=1.0 / NCOL, in1=mean_sq[:],
+                                           op0=ALU.mult, op1=ALU.subtract)
+            nc.vector.tensor_scalar(out=var[:], in0=var[:], scalar1=0.0, scalar2=EPS, op0=ALU.max, op1=ALU.add)
+            nc.gpsimd.tensor_tensor(out=rstd[:], in0=var[:], in1=neg_half[:], op=ALU.pow)
+            if half == 1:
+                return (mean, rstd, None)
+            neg_mean = keep.tile([P, NBT], F32, name="neg_mean")
+            shift = keep.tile([P, NBT], F32, name="shift")
+            nc.vector.tensor_scalar(out=neg_mean[:], in0=mean[:], scalar1=-1.0, scalar2=None, op0=ALU.mult)
+            nc.gpsimd.tensor_tensor(out=shift[:], in0=neg_mean[:], in1=rstd[:], op=ALU.mult)
+            return (mean, rstd, shift)
 
         nc.vector.memset(neg_half[:], -0.5)
         nc.scalar.activation(out=warm[:], in_=neg_half[:, 0:1], func=ACT.Sigmoid)
@@ -129,8 +121,8 @@ def tile_adaptivelstmcell_pb_kernel(
             grouped_pool = stream.enter_context(tc.tile_pool(name="grouped_pool", bufs=3))
             mx_pool = stream.enter_context(tc.tile_pool(name="mx_pool", bufs=2))
             hyper_pool = stream.enter_context(tc.tile_pool(name="hyper_pool", bufs=2))
-            alpha_pool = stream.enter_context(tc.tile_pool(name="alpha_pool", bufs=4))
-            bias_pool = stream.enter_context(tc.tile_pool(name="bias_pool", bufs=2))
+            alpha_pool = stream.enter_context(tc.tile_pool(name="alpha_pool", bufs=3))
+            bias_pool = stream.enter_context(tc.tile_pool(name="bias_pool", bufs=3))
 
             def staged_words(i):
                 return u_hid[:, i * 2048:(i + 1) * 2048]
@@ -172,11 +164,8 @@ def tile_adaptivelstmcell_pb_kernel(
             bias_rows = {}
 
             def copy_waiting():
-                for (engine, out, in_, accum_out) in waiting:
-                    if accum_out is None:
-                        copy_on(engine, out, in_)
-                    else:
-                        nc.scalar.activation(out=out, in_=in_, func=ACT.Copy, accum_out=accum_out)
+                for (engine, out, in_) in waiting:
+                    copy_on(engine, out, in_)
                 waiting[:] = []
 
             homes = [(ps_t, "bank"), (ps_xh, "xh"), (ps_alpha, "alpha_ps"), (ps_beta, "beta_ps")]
@@ -200,7 +189,7 @@ def tile_adaptivelstmcell_pb_kernel(
                         first = (2 * h + r) * 512 + 256 * g
                         nc.tensor.transpose(bank[:, u, r, :], src[:, first + u:first + 2 * P:2], ident_f[:])
                 pairs = grouped[(operand, g)][:].bitcast(F32).rearrange("p (n u) -> p n u", u=2)
-                waiting.append((engine, pairs[:, 256 * h:256 * (h + 1), :], bank[:].rearrange("p u r c -> p (r c) u"), None))
+                waiting.append((engine, pairs[:, 256 * h:256 * (h + 1), :], bank[:].rearrange("p u r c -> p (r c) u")))
 
             def quantise(operand, g, words, scales):
                 nc.vector.quantize_mx(out=words[:, g, :].bitcast(FP8X4), scales=scales[:, g, :],
@@ -213,7 +202,7 @@ def tile_adaptivelstmcell_pb_kernel(
                     for t in range(2):
                         nc.tensor.transpose(bank[:, s, t, :], src[:, 2 * pair + t, s * P:(s + 1) * P], ident_b[:])
                 waiting.append((engine, zT[i][:, 4 * part:4 * part + 4, 256 * pair:256 * (pair + 1)],
-                                bank[:].rearrange("p s t b -> p s (t b)"), None))
+                                bank[:].rearrange("p s t b -> p s (t b)")))
 
             def transpose_hyper(c):
                 bank = new_bank([P, 2, 4, P], BF16)
@@ -221,7 +210,7 @@ def tile_adaptivelstmcell_pb_kernel(
                     for r in range(4):
                         nc.tensor.transpose(bank[:, i, r, :], hyper_raw[c // 2][i][:, (c % 2) * 4 + r, :], ident_b[:])
                 hyper[c] = hyper_pool.tile([P, 2, CH], BF16, name="hyper")
-                waiting.append(("scalar", hyper[c][:], bank[:].rearrange("p i r c -> p i (r c)"), None))
+                waiting.append(("scalar", hyper[c][:], bank[:].rearrange("p i r c -> p i (r c)")))
 
             def transpose_vectors():
                 bank = new_bank([P, 2, P], BF16)
@@ -232,13 +221,15 @@ def tile_adaptivelstmcell_pb_kernel(
                                         in1=vecT[:, COL_LN_H_B:COL_LN_H_B + 32], op=ALU.add)
                 nc.vector.tensor_copy(out=vecT_f[:], in_=vecT[:])
 
-            def spread_bias(c):
-                bank = new_bank([P, 4, P], BF16)
-                for m in range(4):
-                    col = COL_B_IH + 4 * c + m
-                    nc.tensor.transpose(bank[:, m, :], vecT[:, col:col + 1].to_broadcast([P, P]), ident_b[:])
+            def load_bias(c):
                 bias_rows[c] = bias_pool.tile([P, CH], BF16, name="bias_rows")
-                waiting.append(("scalar", bias_rows[c][:], bank[:].rearrange("p m c -> p (m c)"), bias_sum[:, c:c + 1]))
+                nc.sync.dma_start(out=bias_rows[c][:], in_=b_ih[c * CH:(c + 1) * CH].partition_broadcast(P))
+
+            def sum_bias():
+                nc.vector.tensor_reduce(out=bias_part[:], in_=vecT_f[:, COL_B_IH:COL_B_IH + 32], axis=AX.X, op=ALU.add)
+                bank = new_bank([P, P], F32)
+                nc.tensor.transpose(bank[:], bias_part[:].to_broadcast([P, P]), ident_f[:])
+                nc.vector.tensor_reduce(out=bias_total[:], in_=bank[:], axis=AX.X, op=ALU.add)
 
             load_words(staged_words(0), x)
             load_weights(0)
@@ -251,6 +242,8 @@ def tile_adaptivelstmcell_pb_kernel(
                                   (1, COL_LN_I_B - P, ln_i_b), (1, COL_LN_H_B - P, ln_h_b)):
                 nc.sync.dma_start(out=vec_rows[row:row + vec.shape[0] // P, i, :], in_=vec.rearrange("(m p) -> m p", p=P))
             nc.sync.dma_start(out=b_hh_rows[0:NCH, :], in_=b_hh.rearrange("(c n) -> c n", c=NCH))
+            load_bias(0)
+            load_bias(1)
             load_hyper(1)
             load_weights(2)
 
@@ -299,10 +292,9 @@ def tile_adaptivelstmcell_pb_kernel(
             def banks_of_step(n):
                 c = n // NBT
                 r = n % NBT
-                second = "vector" if c < NCH - 1 else "scalar"
+                second = "vector"
                 if n == 0:
                     transpose_vectors()
-                    spread_bias(0)
                     for j in range(4):
                         transpose_words(1, raw[1][:], j, ("scalar", "vector")[j % 2])
                     load_weights(4)
@@ -318,8 +310,10 @@ def tile_adaptivelstmcell_pb_kernel(
                     transpose_hyper(c + 1)
                     if c % 2 == 0:
                         load_hyper(c // 2 + 2)
-                if r == 2 and c + 1 < NCH:
-                    spread_bias(c + 1)
+                if r == 0 and c + 2 < NCH:
+                    load_bias(c + 2)
+                if n == 6:
+                    sum_bias()
                 if 3 <= c <= 6 and r in (0, 3):
                     e = 2 * (c - 3) + r // 3
                     if e < 4:
@@ -568,8 +562,11 @@ def tile_adaptivelstmcell_pb_kernel(
                 cols = slice(hf * CH, (hf + 1) * CH)
                 nc.vector.tensor_tensor(out=hy_of(bt)[:, cols], in0=hy_of(bt)[:, cols], in1=flat(out_rows[(bt, hf)]),
                                         op=ALU.mult)
-                if hf == 1:
-                    nc.sync.dma_start(out=out_0[bt * P:(bt + 1) * P, :], in_=hy_of(bt))
+                nc.sync.dma_start(out=out_0[bt * P:(bt + 1) * P, cols], in_=hy_of(bt)[:, cols])
+
+            def activate_out(k):
+                g = outT[:, 2 * k:2 * k + 2, :].rearrange("p h b -> p (h b)")
+                nc.scalar.activation(out=g, in_=g, func=ACT.Sigmoid)
 
             def cell_norm(bt):
                 cell_scalars(bt, 0)
@@ -586,12 +583,12 @@ def tile_adaptivelstmcell_pb_kernel(
             cell_norm(0)
             cell_norm(1)
             finish_cy(0)
-            for hb in range(NHB // 2):
-                activate((hb, GATE_O))
+            activate_out(0)
+            activate_out(1)
             cell_norm(2)
             finish_cy(1)
-            for hb in range(NHB // 2, NHB):
-                activate((hb, GATE_O))
+            activate_out(2)
+            activate_out(3)
             cell_norm(3)
             finish_cy(2)
             finish_cy(3)

@@ -112,9 +112,9 @@ def tile_adaptivelstmcell_pb_kernel(
         make_identity(nc, ident_b[:])
 
         with ExitStack() as stream:
-            ps_t = stream.enter_context(tc.psum_pool(name="ps_t", bufs=2))
+            ps_t = stream.enter_context(tc.psum_pool(name="ps_t", bufs=3))
             ps_xh = stream.enter_context(tc.psum_pool(name="ps_xh", bufs=2))
-            ps_alpha = stream.enter_context(tc.psum_pool(name="ps_alpha", bufs=2))
+            ps_alpha = stream.enter_context(tc.psum_pool(name="ps_alpha", bufs=1))
             ps_beta = stream.enter_context(tc.psum_pool(name="ps_beta", bufs=2))
             raw_pool = stream.enter_context(tc.tile_pool(name="raw_pool", bufs=3))
             hyper_raw_pool = stream.enter_context(tc.tile_pool(name="hyper_raw_pool", bufs=2))
@@ -172,7 +172,7 @@ def tile_adaptivelstmcell_pb_kernel(
             made = []
 
             def new_bank(shape, dtype):
-                if len(waiting) == 2 * len(homes):
+                if len(waiting) == 3:
                     copy_waiting()
                 made.append(shape)
                 (pool, tag) = homes[len(made) % len(homes)]
@@ -292,7 +292,7 @@ def tile_adaptivelstmcell_pb_kernel(
             def banks_of_step(n):
                 c = n // NBT
                 r = n % NBT
-                second = "vector"
+                second = "scalar"
                 if n == 0:
                     transpose_vectors()
                     for j in range(4):
@@ -310,7 +310,7 @@ def tile_adaptivelstmcell_pb_kernel(
                     transpose_hyper(c + 1)
                     if c % 2 == 0:
                         load_hyper(c // 2 + 2)
-                if r == 0 and c + 2 < NCH:
+                if r == 1 and c + 2 < NCH:
                     load_bias(c + 2)
                 if n == 6:
                     sum_bias()
@@ -345,12 +345,11 @@ def tile_adaptivelstmcell_pb_kernel(
                 nc.scalar.activation(out=unused[:, 0:CH], in_=u, func=ACT.Square,
                                      accum_out=row_sq[:, half, bt, c % NCH:c % NCH + 1])
 
-            def normalise_input_half():
-                for i in range(NCH):
-                    for bt in range(NBT):
-                        cols = u_in[:, bt * NCOL + i * CH:bt * NCOL + (i + 1) * CH]
-                        nc.gpsimd.tensor_scalar(out=cols, in0=cols, scalar1=scal_in[1][:, bt:bt + 1],
-                                                scalar2=scal_in[2][:, bt:bt + 1], op0=ALU.mult, op1=ALU.add)
+            def normalise_input(k):
+                (i, bt) = (k // NBT, k % NBT)
+                cols = u_in[:, bt * NCOL + i * CH:bt * NCOL + (i + 1) * CH]
+                nc.gpsimd.tensor_scalar(out=cols, in0=cols, scalar1=scal_in[1][:, bt:bt + 1],
+                                        scalar2=scal_in[2][:, bt:bt + 1], op0=ALU.mult, op1=ALU.add)
 
             FIRST_HID = NCH * NBT
             scal_in = None
@@ -389,7 +388,10 @@ def tile_adaptivelstmcell_pb_kernel(
                     add_beta(n - 1)
                 if n == FIRST_HID + 2:
                     scal_in = half_scalars(0)
-                    normalise_input_half()
+                if n > FIRST_HID + 2:
+                    normalise_input(n - FIRST_HID - 3)
+            for k in range(NUNIT - FIRST_HID - 3, NCH * NBT):
+                normalise_input(k)
             add_beta(NUNIT - 1)
             for n in range(NUNIT - 2, NUNIT):
                 sum_squares(n)

@@ -27,6 +27,7 @@ GATE_I = 0
 GATE_J = 1
 GATE_F = 2
 GATE_O = 3
+BY_GPSIMD = list(range(NCH)) + list(range(12, 15))
 
 COL_B_IH = 0
 COL_LN_I_W = 32
@@ -35,6 +36,7 @@ COL_LN_C_W = 96
 COL_LN_C_B = 104
 COL_LN_I_B = 128
 COL_LN_H_B = 160
+COL_B_HH = 192
 
 FLOPS = 2 * 2 * B * NCOL * K + 16 * 2 * B * H * 128
 
@@ -64,9 +66,14 @@ def tile_adaptivelstmcell_pb_kernel(
         warm = keep.tile([P, 1], F32, name="warm")
         row_sum = keep.tile([P, 2, NBT, NCH], F32, name="row_sum")
         row_sq = keep.tile([P, 2, NBT, NCH], F32, name="row_sq")
-        bias_part = keep.tile([P, 1], F32, name="bias_part")
-        bias_total = keep.tile([P, 1], F32, name="bias_total")
-        unused = keep.tile([P, H], BF16, name="unused")
+        bias_part = keep.tile([P, 2], F32, name="bias_part")
+        bias_total = keep.tile([P, 2], F32, name="bias_total")
+        unused = keep.tile([P, 4, CH], BF16, name="unused")
+        sums_made = []
+
+        def unused_place():
+            sums_made.append(None)
+            return unused[:, len(sums_made) % 4, :]
 
         def copy_on(engine, out, in_):
             if engine == "scalar":
@@ -88,7 +95,7 @@ def tile_adaptivelstmcell_pb_kernel(
             var = keep.tile([P, NBT], F32, name="var%d" % half)
             rstd = keep.tile([P, NBT], F32, name="rstd%d" % half)
             nc.vector.tensor_reduce(out=total[:], in_=row_sum[:, half, :, :], axis=AX.X, op=ALU.add)
-            nc.vector.tensor_scalar(out=mean[:], in0=total[:], scalar1=bias_total[:] if half == 0 else 0.0, scalar2=1.0 / NCOL,
+            nc.vector.tensor_scalar(out=mean[:], in0=total[:], scalar1=bias_total[:, half:half + 1], scalar2=1.0 / NCOL,
                                     op0=ALU.add, op1=ALU.mult)
             nc.vector.tensor_tensor(out=mean_sq[:], in0=mean[:], in1=mean[:], op=ALU.mult)
             nc.vector.tensor_reduce(out=total_sq[:], in_=row_sq[:, half, :, :], axis=AX.X, op=ALU.add)
@@ -223,13 +230,18 @@ def tile_adaptivelstmcell_pb_kernel(
 
             def load_bias(c):
                 bias_rows[c] = bias_pool.tile([P, CH], BF16, name="bias_rows")
-                nc.sync.dma_start(out=bias_rows[c][:], in_=b_ih[c * CH:(c + 1) * CH].partition_broadcast(P))
+                src = b_ih if c < NCH else b_hh
+                nc.sync.dma_start(out=bias_rows[c][:], in_=src[c % NCH * CH:(c % NCH + 1) * CH].partition_broadcast(P))
 
-            def sum_bias():
-                nc.vector.tensor_reduce(out=bias_part[:], in_=vecT_f[:, COL_B_IH:COL_B_IH + 32], axis=AX.X, op=ALU.add)
+            def sum_bias(half):
+                own = [c for c in BY_GPSIMD if c // NCH == half]
+                col = (COL_B_IH, COL_B_HH)[half]
+                cols = vecT_f[:, col + 4 * (own[0] % NCH):col + 4 * (own[-1] % NCH + 1)]
+                one = slice(half, half + 1)
+                nc.vector.tensor_reduce(out=bias_part[:, one], in_=cols, axis=AX.X, op=ALU.add)
                 bank = new_bank([P, P], F32)
-                nc.tensor.transpose(bank[:], bias_part[:].to_broadcast([P, P]), ident_f[:])
-                nc.vector.tensor_reduce(out=bias_total[:], in_=bank[:], axis=AX.X, op=ALU.add)
+                nc.tensor.transpose(bank[:], bias_part[:, one].to_broadcast([P, P]), ident_f[:])
+                nc.vector.tensor_reduce(out=bias_total[:, one], in_=bank[:], axis=AX.X, op=ALU.add)
 
             load_words(staged_words(0), x)
             load_weights(0)
@@ -239,7 +251,7 @@ def tile_adaptivelstmcell_pb_kernel(
             load_weights(1)
             for (i, row, vec) in ((0, COL_B_IH, b_ih), (0, COL_LN_I_W, ln_i_w), (0, COL_LN_H_W, ln_h_w),
                                   (0, COL_LN_C_W, ln_c_w), (0, COL_LN_C_B, ln_c_b),
-                                  (1, COL_LN_I_B - P, ln_i_b), (1, COL_LN_H_B - P, ln_h_b)):
+                                  (1, COL_LN_I_B - P, ln_i_b), (1, COL_LN_H_B - P, ln_h_b), (1, COL_B_HH - P, b_hh)):
                 nc.sync.dma_start(out=vec_rows[row:row + vec.shape[0] // P, i, :], in_=vec.rearrange("(m p) -> m p", p=P))
             nc.sync.dma_start(out=b_hh_rows[0:NCH, :], in_=b_hh.rearrange("(c n) -> c n", c=NCH))
             load_bias(0)
@@ -310,10 +322,10 @@ def tile_adaptivelstmcell_pb_kernel(
                     transpose_hyper(c + 1)
                     if c % 2 == 0:
                         load_hyper(c // 2 + 2)
-                if r == 1 and c + 2 < NCH:
+                if r == 1 and c + 2 in BY_GPSIMD[2:]:
                     load_bias(c + 2)
-                if n == 6:
-                    sum_bias()
+                if n in (6, 7):
+                    sum_bias(n - 6)
                 if 3 <= c <= 6 and r in (0, 3):
                     e = 2 * (c - 3) + r // 3
                     if e < 4:
@@ -337,12 +349,12 @@ def tile_adaptivelstmcell_pb_kernel(
                 (c, bt, half, u) = where(n)
                 nc.vector.scalar_tensor_tensor(out=u, in0=u, scalar=1.0, in1=beta_ps[n][:], op0=ALU.mult, op1=ALU.add,
                                                accum_out=row_sum[:, half, bt, c % NCH:c % NCH + 1])
-                if half == 0:
+                if c in BY_GPSIMD:
                     nc.gpsimd.tensor_tensor(out=u, in0=u, in1=bias_rows[c][:], op=ALU.add)
 
             def sum_squares(n):
                 (c, bt, half, u) = where(n)
-                nc.scalar.activation(out=unused[:, 0:CH], in_=u, func=ACT.Square,
+                nc.scalar.activation(out=unused_place(), in_=u, func=ACT.Square,
                                      accum_out=row_sq[:, half, bt, c % NCH:c % NCH + 1])
 
             def normalise_input(k):
@@ -353,6 +365,13 @@ def tile_adaptivelstmcell_pb_kernel(
 
             FIRST_HID = NCH * NBT
             scal_in = None
+
+            def pieces(n):
+                (first, end) = (FIRST_HID + 3, BY_GPSIMD[NCH] * NBT)
+                if not first <= n < end:
+                    return []
+                return range(NCH * NBT * (n - first) // (end - first), NCH * NBT * (n - first + 1) // (end - first))
+
             alpha_of(0)
             for n in range(NUNIT):
                 (c, bt, half, u) = where(n)
@@ -374,24 +393,21 @@ def tile_adaptivelstmcell_pb_kernel(
                 banks_of_step(n)
                 beta_ps[n] = ps_beta.tile([P, CH], F32, name="beta_ps")
                 nc.tensor.matmul(beta_ps[n][:], lhsT=zT[1][:, c // 2, rows], rhs=hyper[c][:, 1, :], start=True,
-                                 stop=(half == 0))
-                if half == 1:
+                                 stop=(c in BY_GPSIMD))
+                if c not in BY_GPSIMD:
                     nc.tensor.matmul(beta_ps[n][:], lhsT=ident_b[:, c % NCH:c % NCH + 1].to_broadcast([P, P]),
                                      rhs=b_hh_rows[:], start=False, stop=True)
-                if 3 <= n < FIRST_HID + 3:
-                    sum_squares(n - 3)
-                if n >= FIRST_HID + 2:
-                    sum_squares(n - 2)
+                for k in (n - 3, n - 2):
+                    if k >= 0 and (where(k)[0] in BY_GPSIMD) == (k == n - 3):
+                        sum_squares(k)
                 quantise_in_step(n)
                 nc.vector.tensor_tensor(out=u, in0=xh[:], in1=alpha_sb[n][:], op=ALU.mult)
                 if n >= 1:
                     add_beta(n - 1)
                 if n == FIRST_HID + 2:
                     scal_in = half_scalars(0)
-                if n > FIRST_HID + 2:
-                    normalise_input(n - FIRST_HID - 3)
-            for k in range(NUNIT - FIRST_HID - 3, NCH * NBT):
-                normalise_input(k)
+                for k in pieces(n):
+                    normalise_input(k)
             add_beta(NUNIT - 1)
             for n in range(NUNIT - 2, NUNIT):
                 sum_squares(n)
@@ -526,12 +542,12 @@ def tile_adaptivelstmcell_pb_kernel(
 
             def cell_sums(bt, hf):
                 row = flat(cell_rows[(bt, hf)])
-                nc.scalar.activation(out=unused[:, CH:2 * CH], in_=row, func=ACT.Square, scale=1.0 / 32.0,
+                nc.scalar.activation(out=unused_place(), in_=row, func=ACT.Square, scale=1.0 / 32.0,
                                      accum_out=cell_sq[:, bt, hf:hf + 1])
                 if bt < 2:
                     nc.vector.tensor_reduce(out=cell_sum[:, bt, hf:hf + 1], in_=row, axis=AX.X, op=ALU.add)
                 else:
-                    nc.scalar.activation(out=unused[:, 0:CH], in_=row, func=ACT.Copy, accum_out=cell_sum[:, bt, hf:hf + 1])
+                    nc.scalar.activation(out=unused_place(), in_=row, func=ACT.Copy, accum_out=cell_sum[:, bt, hf:hf + 1])
 
             def cell_scalars(bt, stage):
                 one = slice(bt, bt + 1)

from contextlib import ExitStack

import concourse.mybir as mybir
from concourse.masks import make_identity

F32 = mybir.dt.float32
BF16 = mybir.dt.bfloat16
U32 = mybir.dt.uint32
U8 = mybir.dt.uint8
FP8X4 = mybir.dt.float8_e4m3fn_x4
ALU = mybir.AluOpType
ACT = mybir.ActivationFunctionType
AX = mybir.AxisListType

P = 128
B = 512
K = 1024
H = 1024
NBT = B // P
NCOL = 4 * H
CH = 512
NCH = NCOL // CH
NUNIT = 2 * NCH * NBT
NHB = H // P
EPS = 1e-5
GATE_I = 0
GATE_J = 1
GATE_F = 2
GATE_O = 3
BY_GPSIMD = list(range(NCH)) + list(range(12, 15))

COL_B_IH = 0
COL_LN_I_W = 32
COL_LN_H_W = 64
COL_LN_C_W = 96
COL_LN_C_B = 104
COL_LN_I_B = 128
COL_LN_H_B = 160
COL_B_HH = 192

FLOPS = 2 * 2 * B * NCOL * K + 16 * 2 * B * H * 128


def tile_adaptivelstmcell_pb_kernel(
    tc, x, hx, cx, zw, zb, w_ih, w_hh, b_ih, b_hh, norm_alpha_w, bias_beta_w,
    ln_i_w, ln_i_b, ln_h_w, ln_h_b, ln_c_w, ln_c_b, out_0, out_1,
):
    nc = tc.nc
    with ExitStack() as whole:
        whole.enter_context(tc.manual_schedule())
        keep = whole.enter_context(tc.tile_pool(name="keep", bufs=1))

        u_in = keep.tile([P, NBT * NCOL], F32, name="u_in")
        u_hid = keep.tile([P, NBT * NCOL], F32, name="u_hid")
        ident_f = keep.tile([P, P], F32, name="ident_f")
        ident_b = keep.tile([P, P], BF16, name="ident_b")
        act_words = [keep.tile([P, 2, B], U32, name="act_words%d" % h, align_bytes=64) for h in range(2)]
        act_scales = [keep.tile([P, 2, B], U8, name="act_scales%d" % h, align_bytes=64) for h in range(2)]
        zT = [keep.tile([P, 8, B], BF16, name="zT%d" % i) for i in range(2)]
        b_hh_rows = keep.tile([P, CH], BF16, name="b_hh_rows")
        vec_rows = keep.tile([P, 2, P], BF16, name="vec_rows")
        vecT = keep.tile([P, 2 * P], BF16, name="vecT")
        vecT_f = keep.tile([P, 2 * P], F32, name="vecT_f")
        shiftT = keep.tile([P, 32], F32, name="shiftT")
        neg_half = keep.tile([P, NBT], F32, name="neg_half")
        warm = keep.tile([P, 1], F32, name="warm")
        row_sum = keep.tile([P, 2, NBT, NCH], F32, name="row_sum")
        row_sq = keep.tile([P, 2, NBT, NCH], F32, name="row_sq")
        bias_part = keep.tile([P, 2], F32, name="bias_part")
        bias_total = keep.tile([P, 2], F32, name="bias_total")
        unused = keep.tile([P, 4, CH], BF16, name="unused")
        sums_made = []

        def unused_place():
            sums_made.append(None)
            return unused[:, len(sums_made) % 4, :]

        def copy_on(engine, out, in_):
            if engine == "scalar":
                nc.scalar.copy(out=out, in_=in_)
            else:
                nc.vector.tensor_copy(out=out, in_=in_)

        def rows_on_partitions(ap2d):
            return ap2d.rearrange("(r p) k -> p r k", p=P)

        def flat(t):
            return t[:].rearrange("p b c -> p (b c)")

        def half_scalars(half):
            total = keep.tile([P, NBT], F32, name="total%d" % half)
            total_sq = keep.tile([P, NBT], F32, name="total_sq%d" % half)
            mean = keep.tile([P, NBT], F32, name="mean%d" % half)
            mean_sq = keep.tile([P, NBT], F32, name="mean_sq%d" % half)
            var = keep.tile([P, NBT], F32, name="var%d" % half)
            rstd = keep.tile([P, NBT], F32, name="rstd%d" % half)
            nc.vector.tensor_reduce(out=total[:], in_=row_sum[:, half, :, :], axis=AX.X, op=ALU.add)
            nc.vector.tensor_scalar(out=mean[:], in0=total[:], scalar1=bias_total[:, half:half + 1], scalar2=1.0 / NCOL,
                                    op0=ALU.add, op1=ALU.mult)
            nc.vector.tensor_tensor(out=mean_sq[:], in0=mean[:], in1=mean[:], op=ALU.mult)
            nc.vector.tensor_reduce(out=total_sq[:], in_=row_sq[:, half, :, :], axis=AX.X, op=ALU.add)
            nc.vector.scalar_tensor_tensor(out=var[:], in0=total_sq[:], scalar=1.0 / NCOL, in1=mean_sq[:],
                                           op0=ALU.mult, op1=ALU.subtract)
            nc.vector.tensor_scalar(out=var[:], in0=var[:], scalar1=0.0, scalar2=EPS, op0=ALU.max, op1=ALU.add)
            nc.gpsimd.tensor_tensor(out=rstd[:], in0=var[:], in1=neg_half[:], op=ALU.pow)
            if half == 1:
                return (mean, rstd, None)
            neg_mean = keep.tile([P, NBT], F32, name="neg_mean")
            shift = keep.tile([P, NBT], F32, name="shift")
            nc.vector.tensor_scalar(out=neg_mean[:], in0=mean[:], scalar1=-1.0, scalar2=None, op0=ALU.mult)
            nc.gpsimd.tensor_tensor(out=shift[:], in0=neg_mean[:], in1=rstd[:], op=ALU.mult)
            return (mean, rstd, shift)

        nc.vector.memset(neg_half[:], -0.5)
        nc.scalar.activation(out=warm[:], in_=neg_half[:, 0:1], func=ACT.Sigmoid)
        nc.vector.memset(vec_rows[:], 0.0)
        nc.vector.memset(b_hh_rows[:], 0.0)
        make_identity(nc, ident_f[:])
        make_identity(nc, ident_b[:])

        with ExitStack() as stream:
            ps_t = stream.enter_context(tc.psum_pool(name="ps_t", bufs=3))
            ps_xh = stream.enter_context(tc.psum_pool(name="ps_xh", bufs=2))
            ps_alpha = stream.enter_context(tc.psum_pool(name="ps_alpha", bufs=1))
            ps_beta = stream.enter_context(tc.psum_pool(name="ps_beta", bufs=2))
            raw_pool = stream.enter_context(tc.tile_pool(name="raw_pool", bufs=3))
            hyper_raw_pool = stream.enter_context(tc.tile_pool(name="hyper_raw_pool", bufs=2))
            grouped_pool = stream.enter_context(tc.tile_pool(name="grouped_pool", bufs=3))
            mx_pool = stream.enter_context(tc.tile_pool(name="mx_pool", bufs=2))
            hyper_pool = stream.enter_context(tc.tile_pool(name="hyper_pool", bufs=2))
            alpha_pool = stream.enter_context(tc.tile_pool(name="alpha_pool", bufs=3))
            bias_pool = stream.enter_context(tc.tile_pool(name="bias_pool", bufs=3))

            def staged_words(i):
                return u_hid[:, i * 2048:(i + 1) * 2048]

            def staged_z(i, part):
                first = 4096 + (2 * i + part) * 1024
                return u_hid[:, first:first + 1024].bitcast(BF16).rearrange("p (r k) -> p r k", r=NBT)

            z_rows = [rows_on_partitions(z.rearrange("b s a -> b (s a)")) for z in (zw, zb)]

            def load_words(dst, src):
                nc.sync.dma_start(out=dst.bitcast(BF16).rearrange("p (r k) -> p r k", r=4), in_=rows_on_partitions(src))

            def load_z(i, part):
                nc.sync.dma_start(out=staged_z(i, part), in_=z_rows[i][:, :, 512 * part:512 * (part + 1)])

            raw = {}
            hyper_raw = {}

            def load_weights(c):
                if c < 2 * NCH:
                    w = w_ih if c < NCH else w_hh
                    raw[c] = raw_pool.tile([P, 2048], F32, name="raw")
                    load_words(raw[c][:], w[(c % NCH) * CH:(c % NCH + 1) * CH, :])

            def load_hyper(s):
                if s < 8:
                    ra = hyper_raw_pool.tile([P, 8, P], BF16, name="raw_alpha")
                    rb = hyper_raw_pool.tile([P, 8, P], BF16, name="raw_beta")
                    nc.sync.dma_start(out=ra[:], in_=norm_alpha_w[s, :, :].rearrange("(r p) a -> p r a", p=P))
                    nc.sync.dma_start(out=rb[:], in_=bias_beta_w[s, :, :].rearrange("(r p) a -> p r a", p=P))
                    hyper_raw[s] = (ra, rb)

            waiting = []
            grouped = {}
            w_words = {}
            w_scales = {}
            hyper = {}
            bias_rows = {}

            def copy_waiting():
                for (engine, out, in_) in waiting:
                    copy_on(engine, out, in_)
                waiting[:] = []

            homes = [(ps_t, "bank"), (ps_xh, "xh"), (ps_alpha, "alpha_ps"), (ps_beta, "beta_ps")]
            made = []

            def new_bank(shape, dtype):
                if len(waiting) == 3:
                    copy_waiting()
                made.append(shape)
                (pool, tag) = homes[len(made) % len(homes)]
                return pool.tile(shape, dtype, name=tag)

            def transpose_words(operand, src, j, engine):
                g = j // 2
                h = j % 2
                if h == 0:
                    grouped[(operand, g)] = grouped_pool.tile([P, 4 * CH], BF16, name="grouped", align_bytes=64)
                bank = new_bank([P, 2, 2, P], F32)
                for u in range(2):
                    for r in range(2):
                        first = (2 * h + r) * 512 + 256 * g
                        nc.tensor.transpose(bank[:, u, r, :], src[:, first + u:first + 2 * P:2], ident_f[:])
                pairs = grouped[(operand, g)][:].bitcast(F32).rearrange("p (n u) -> p n u", u=2)
                waiting.append((engine, pairs[:, 256 * h:256 * (h + 1), :], bank[:].rearrange("p u r c -> p (r c) u")))

            def quantise(operand, g, words, scales):
                nc.vector.quantize_mx(out=words[:, g, :].bitcast(FP8X4), scales=scales[:, g, :],
                                      in_=grouped[(operand, g)][:])

            def transpose_z(i, part, pair, engine):
                src = staged_z(i, part)
                bank = new_bank([P, 4, 2, P], BF16)
                for s in range(4):
                    for t in range(2):
                        nc.tensor.transpose(bank[:, s, t, :], src[:, 2 * pair + t, s * P:(s + 1) * P], ident_b[:])
                waiting.append((engine, zT[i][:, 4 * part:4 * part + 4, 256 * pair:256 * (pair + 1)],
                                bank[:].rearrange("p s t b -> p s (t b)")))

            def transpose_hyper(c):
                bank = new_bank([P, 2, 4, P], BF16)
                for i in range(2):
                    for r in range(4):
                        nc.tensor.transpose(bank[:, i, r, :], hyper_raw[c // 2][i][:, (c % 2) * 4 + r, :], ident_b[:])
                hyper[c] = hyper_pool.tile([P, 2, CH], BF16, name="hyper")
                waiting.append(("scalar", hyper[c][:], bank[:].rearrange("p i r c -> p i (r c)")))

            def transpose_vectors():
                bank = new_bank([P, 2, P], BF16)
                for i in range(2):
                    nc.tensor.transpose(bank[:, i, :], vec_rows[:, i, :], ident_b[:])
                nc.vector.tensor_copy(out=vecT[:], in_=bank[:].rearrange("p i c -> p (i c)"))
                nc.vector.tensor_tensor(out=shiftT[:], in0=vecT[:, COL_LN_I_B:COL_LN_I_B + 32],
                                        in1=vecT[:, COL_LN_H_B:COL_LN_H_B + 32], op=ALU.add)
                nc.vector.tensor_copy(out=vecT_f[:], in_=vecT[:])

            def load_bias(c):
                bias_rows[c] = bias_pool.tile([P, CH], BF16, name="bias_rows")
                src = b_ih if c < NCH else b_hh
                nc.sync.dma_start(out=bias_rows[c][:], in_=src[c % NCH * CH:(c % NCH + 1) * CH].partition_broadcast(P))

            def sum_bias(half):
                own = [c for c in BY_GPSIMD if c // NCH == half]
                col = (COL_B_IH, COL_B_HH)[half]
                cols = vecT_f[:, col + 4 * (own[0] % NCH):col + 4 * (own[-1] % NCH + 1)]
                one = slice(half, half + 1)
                nc.vector.tensor_reduce(out=bias_part[:, one], in_=cols, axis=AX.X, op=ALU.add)
                bank = new_bank([P, P], F32)
                nc.tensor.transpose(bank[:], bias_part[:, one].to_broadcast([P, P]), ident_f[:])
                nc.vector.tensor_reduce(out=bias_total[:, one], in_=bank[:], axis=AX.X, op=ALU.add)

            load_words(staged_words(0), x)
            load_weights(0)
            load_z(0, 0)
            load_z(1, 0)
            load_hyper(0)
            load_weights(1)
            for (i, row, vec) in ((0, COL_B_IH, b_ih), (0, COL_LN_I_W, ln_i_w), (0, COL_LN_H_W, ln_h_w),
                                  (0, COL_LN_C_W, ln_c_w), (0, COL_LN_C_B, ln_c_b),
                                  (1, COL_LN_I_B - P, ln_i_b), (1, COL_LN_H_B - P, ln_h_b), (1, COL_B_HH - P, b_hh)):
                nc.sync.dma_start(out=vec_rows[row:row + vec.shape[0] // P, i, :], in_=vec.rearrange("(m p) -> m p", p=P))
            nc.sync.dma_start(out=b_hh_rows[0:NCH, :], in_=b_hh.rearrange("(c n) -> c n", c=NCH))
            load_bias(0)
            load_bias(1)
            load_hyper(1)
            load_weights(2)

            def new_mx_tiles(c):
                w_words[c] = mx_pool.tile([P, 2, CH], U32, name="w_words", align_bytes=64)
                w_scales[c] = mx_pool.tile([P, 2, CH], U8, name="w_scales", align_bytes=64)

            new_mx_tiles(0)
            for j in range(4):
                transpose_words("x", staged_words(0), j, ("scalar", "vector")[j % 2])
                copy_waiting()
            for j in range(4):
                transpose_words(0, raw[0][:], j, ("scalar", "vector")[j % 2])
                copy_waiting()
                if j % 2 == 1:
                    quantise("x", j // 2, act_words[0], act_scales[0])
            load_weights(3)
            for i in range(2):
                transpose_z(i, 0, 0, "scalar")
                transpose_z(i, 0, 1, "vector")
                copy_waiting()
                quantise(0, i, w_words[0], w_scales[0])
            transpose_hyper(0)
            copy_waiting()
            homes[:] = homes[0:1]

            alpha_ps = {}
            alpha_sb = {}
            beta_ps = {}

            def where(n):
                c = n // NBT
                bt = n % NBT
                half = c // NCH
                first = bt * NCOL + (c % NCH) * CH
                return (c, bt, half, (u_in, u_hid)[half][:, first:first + CH])

            def alpha_of(n):
                (c, bt, half, u) = where(n)
                alpha_ps[n] = ps_alpha.tile([P, CH], F32, name="alpha_ps")
                nc.tensor.matmul(alpha_ps[n][:], lhsT=zT[0][:, c // 2, bt * P:(bt + 1) * P], rhs=hyper[c][:, 0, :],
                                 start=True, stop=True)
                alpha_sb[n] = alpha_pool.tile([P, CH], F32, name="alpha_sb")
                nc.scalar.copy(out=alpha_sb[n][:], in_=alpha_ps[n][:])

            def banks_of_step(n):
                c = n // NBT
                r = n % NBT
                second = "scalar"
                if n == 0:
                    transpose_vectors()
                    for j in range(4):
                        transpose_words(1, raw[1][:], j, ("scalar", "vector")[j % 2])
                    load_weights(4)
                    load_words(staged_words(1), hx)
                    load_z(0, 1)
                    load_z(1, 1)
                elif r == 0 and c + 1 < 2 * NCH:
                    transpose_words(c + 1, raw[c + 1][:], 3, "scalar")
                    load_weights(c + 4)
                elif r > 0 and c + 2 < 2 * NCH:
                    transpose_words(c + 2, raw[c + 2][:], r - 1, ("scalar", second, "scalar")[r - 1])
                if r == 1 and c + 1 < 2 * NCH:
                    transpose_hyper(c + 1)
                    if c % 2 == 0:
                        load_hyper(c // 2 + 2)
                if r == 1 and c + 2 in BY_GPSIMD[2:]:
                    load_bias(c + 2)
                if n in (6, 7):
                    sum_bias(n - 6)
                if 3 <= c <= 6 and r in (0, 3):
                    e = 2 * (c - 3) + r // 3
                    if e < 4:
                        transpose_words("hx", staged_words(1), e, ("scalar", "vector")[e % 2])
                    else:
                        transpose_z((e - 4) // 2, 1, e % 2, ("scalar", "vector")[e % 2])

            def quantise_in_step(n):
                c = n // NBT
                r = n % NBT
                if c + 1 < 2 * NCH and n > 0:
                    if r == (1 if c == 0 else 0):
                        new_mx_tiles(c + 1)
                        quantise(c + 1, 0, w_words[c + 1], w_scales[c + 1])
                    if r == 2:
                        quantise(c + 1, 1, w_words[c + 1], w_scales[c + 1])
                if r == 1 and c in (4, 5):
                    quantise("hx", c - 4, act_words[1], act_scales[1])

            def add_beta(n):
                (c, bt, half, u) = where(n)
                nc.vector.scalar_tensor_tensor(out=u, in0=u, scalar=1.0, in1=beta_ps[n][:], op0=ALU.mult, op1=ALU.add,
                                               accum_out=row_sum[:, half, bt, c % NCH:c % NCH + 1])
                if c in BY_GPSIMD:
                    nc.gpsimd.tensor_tensor(out=u, in0=u, in1=bias_rows[c][:], op=ALU.add)

            def sum_squares(n):
                (c, bt, half, u) = where(n)
                nc.scalar.activation(out=unused_place(), in_=u, func=ACT.Square,
                                     accum_out=row_sq[:, half, bt, c % NCH:c % NCH + 1])

            def normalise_input(k):
                (i, bt) = (k // NBT, k % NBT)
                cols = u_in[:, bt * NCOL + i * CH:bt * NCOL + (i + 1) * CH]
                nc.gpsimd.tensor_scalar(out=cols, in0=cols, scalar1=scal_in[1][:, bt:bt + 1],
                                        scalar2=scal_in[2][:, bt:bt + 1], op0=ALU.mult, op1=ALU.add)

            FIRST_HID = NCH * NBT
            scal_in = None

            def pieces(n):
                (first, end) = (FIRST_HID + 3, BY_GPSIMD[NCH] * NBT)
                if not first <= n < end:
                    return []
                return range(NCH * NBT * (n - first) // (end - first), NCH * NBT * (n - first + 1) // (end - first))

            alpha_of(0)
            for n in range(NUNIT):
                (c, bt, half, u) = where(n)
                rows = slice(bt * P, (bt + 1) * P)
                xh = ps_xh.tile([P, CH], F32, name="xh")
                for g in range(2):
                    nc.tensor.matmul_mx(
                        out=xh[:],
                        lhsT=act_words[half][:, g, rows].bitcast(FP8X4),
                        lhsT_scale=act_scales[half][:, g, rows],
                        rhs=w_words[c][:, g, :].bitcast(FP8X4),
                        rhs_scale=w_scales[c][:, g, :],
                        start=(g == 0),
                        stop=(g == 1),
                    )
                copy_waiting()
                if n + 1 < NUNIT:
                    alpha_of(n + 1)
                banks_of_step(n)
                beta_ps[n] = ps_beta.tile([P, CH], F32, name="beta_ps")
                nc.tensor.matmul(beta_ps[n][:], lhsT=zT[1][:, c // 2, rows], rhs=hyper[c][:, 1, :], start=True,
                                 stop=(c in BY_GPSIMD))
                if c not in BY_GPSIMD:
                    nc.tensor.matmul(beta_ps[n][:], lhsT=ident_b[:, c % NCH:c % NCH + 1].to_broadcast([P, P]),
                                     rhs=b_hh_rows[:], start=False, stop=True)
                for k in (n - 3, n - 2):
                    if k >= 0 and (where(k)[0] in BY_GPSIMD) == (k == n - 3):
                        sum_squares(k)
                quantise_in_step(n)
                nc.vector.tensor_tensor(out=u, in0=xh[:], in1=alpha_sb[n][:], op=ALU.mult)
                if n >= 1:
                    add_beta(n - 1)
                if n == FIRST_HID + 2:
                    scal_in = half_scalars(0)
                for k in pieces(n):
                    normalise_input(k)
            add_beta(NUNIT - 1)
            for n in range(NUNIT - 2, NUNIT):
                sum_squares(n)
            scal_hid = half_scalars(1)

        with ExitStack() as tail:
            tail_keep = tail.enter_context(tc.tile_pool(name="tail_keep", bufs=1))
            part_pool = tail.enter_context(tc.tile_pool(name="part_pool", bufs=3))
            gate_pool = tail.enter_context(tc.tile_pool(name="gate_pool", bufs=2))
            ps_a = tail.enter_context(tc.psum_pool(name="ps_a", bufs=4))
            ps_b = tail.enter_context(tc.psum_pool(name="ps_b", bufs=2))
            ps_c = tail.enter_context(tc.psum_pool(name="ps_c", bufs=2))
            cx_rows = tail_keep.tile([P, NBT, H], BF16, name="cx_rows")
            nc.sync.dma_start(out=cx_rows[:], in_=rows_on_partitions(cx))
            ln_c_w_rows = tail_keep.tile([P, H], BF16, name="ln_c_w_rows")
            ln_c_b_rows = tail_keep.tile([P, H], BF16, name="ln_c_b_rows")
            cellT = tail_keep.tile([P, NHB, B], F32, name="cellT")
            outT = tail_keep.tile([P, NHB, B], F32, name="outT")

            in_T = {}
            hid_T = {}
            hid_part = {}
            gate = {}
            cxT = {}

            def normalise_hidden_half(hb):
                for bt in range(NBT):
                    cols = u_hid[:, bt * NCOL:(bt + 1) * NCOL].rearrange("p (q h) -> p q h", q=4)[:, :, hb * P:(hb + 1) * P]
                    nc.vector.tensor_scalar(out=cols, in0=cols, scalar1=scal_hid[0][:, bt:bt + 1],
                                            scalar2=scal_hid[1][:, bt:bt + 1], op0=ALU.subtract, op1=ALU.mult)

            def columns_to_partitions(key, src, pool, store):
                (hb, q) = key
                store[key] = pool.tile([P, NBT, P], F32, name="turned")
                for bt in range(NBT):
                    first = bt * NCOL + q * H + hb * P
                    nc.tensor.transpose(store[key][:, bt, :], src[:, first:first + P], ident_f[:])

            def turn_cx(hb):
                cxT[hb] = ps_c.tile([P, NBT, P], BF16, name="turned")
                for bt in range(NBT):
                    nc.tensor.transpose(cxT[hb][:, bt, :], cx_rows[:, bt, hb * P:(hb + 1) * P], ident_b[:])

            def hidden_part(key):
                (hb, q) = key
                m = q * NHB + hb
                if q == GATE_O:
                    hid_part[key] = outT[:, hb, :]
                else:
                    t = part_pool.tile([P, B], F32, name="part")
                    hid_part[key] = t[:]
                nc.scalar.activation(out=hid_part[key], in_=flat(hid_T[key]), func=ACT.Identity,
                                     scale=vecT_f[:, COL_LN_H_W + m:COL_LN_H_W + m + 1], bias=shiftT[:, m:m + 1])

            def pre_activation(key):
                (hb, q) = key
                m = q * NHB + hb
                if q == GATE_O:
                    gate[key] = outT[:, hb, :]
                else:
                    t = gate_pool.tile([P, B], F32, name="gate%d" % q)
                    gate[key] = t[:]
                nc.vector.scalar_tensor_tensor(out=gate[key], in0=flat(in_T[key]),
                                               scalar=vecT_f[:, COL_LN_I_W + m:COL_LN_I_W + m + 1], in1=hid_part[key],
                                               op0=ALU.mult, op1=ALU.add)

            def activate(key):
                nc.scalar.activation(out=gate[key], in_=gate[key], func=(ACT.Tanh if key[1] == GATE_J else ACT.Sigmoid))

            def forget_times_cx(hb):
                nc.vector.tensor_tensor(out=gate[(hb, GATE_F)], in0=gate[(hb, GATE_F)], in1=flat(cxT[hb]), op=ALU.mult)

            def new_cell(hb):
                engine = nc.gpsimd if hb < NHB - 1 else nc.vector
                engine.tensor_tensor(out=gate[(hb, GATE_I)], in0=gate[(hb, GATE_I)], in1=gate[(hb, GATE_J)], op=ALU.mult)
                engine.tensor_tensor(out=cellT[:, hb, :], in0=gate[(hb, GATE_F)], in1=gate[(hb, GATE_I)], op=ALU.add)

            def spread_row(col, dst):
                bank = ps_c.tile([P, 8, P], BF16, name="turned")
                for m in range(8):
                    nc.tensor.transpose(bank[:, m, :], vecT[:, col + m:col + m + 1].to_broadcast([P, P]), ident_b[:])
                nc.scalar.copy(out=dst, in_=bank[:].rearrange("p m c -> p (m c)"))

            items = [(hb, q) for hb in range(NHB) for q in (GATE_F, GATE_I, GATE_J, GATE_O)]
            spread_row(COL_LN_C_W, ln_c_w_rows[:])
            spread_row(COL_LN_C_B, ln_c_b_rows[:])
            columns_to_partitions(items[0], u_in, ps_a, in_T)
            columns_to_partitions(items[1], u_in, ps_a, in_T)
            normalise_hidden_half(0)
            normalise_hidden_half(1)
            for t in range(-2, len(items) + 1):
                if t + 2 < len(items):
                    key = items[t + 2]
                    if t + 2 >= 2:
                        columns_to_partitions(key, u_in, ps_a, in_T)
                    columns_to_partitions(key, u_hid, ps_b, hid_T)
                    if key[1] == GATE_J:
                        turn_cx(key[0])
                if 0 <= t + 1 < len(items):
                    hidden_part(items[t + 1])
                if t >= 1 and items[t - 1][1] != GATE_O:
                    activate(items[t - 1])
                    if items[t - 1][1] == GATE_J:
                        new_cell(items[t - 1][0])
                if 0 <= t < len(items):
                    (hb, q) = items[t]
                    pre_activation(items[t])
                    if q == GATE_J:
                        forget_times_cx(hb)
                        if hb + 2 < NHB:
                            normalise_hidden_half(hb + 2)

            cell_sum = keep.tile([P, NBT, 2], F32, name="cell_sum")
            cell_sq = keep.tile([P, NBT, 2], F32, name="cell_sq")
            cell_mean = keep.tile([P, NBT], F32, name="cell_mean")
            cell_msq = keep.tile([P, NBT], F32, name="cell_msq")
            cell_var = keep.tile([P, NBT], F32, name="cell_var")
            cell_rstd = keep.tile([P, NBT], F32, name="cell_rstd")
            cell_rows = {}
            out_rows = {}

            def cy_of(bt):
                return u_in[:, bt * NCOL:bt * NCOL + H]

            def hy_of(bt):
                return u_in[:, bt * NCOL + H:bt * NCOL + 2 * H]

            def rows_to_partitions(bt, hf, src, pool, store):
                store[(bt, hf)] = pool.tile([P, 4, P], F32, name="turned")
                for i in range(4):
                    nc.tensor.transpose(store[(bt, hf)][:, i, :], src[:, 4 * hf + i, bt * P:(bt + 1) * P], ident_f[:])

            def cell_sums(bt, hf):
                row = flat(cell_rows[(bt, hf)])
                nc.scalar.activation(out=unused_place(), in_=row, func=ACT.Square, scale=1.0 / 32.0,
                                     accum_out=cell_sq[:, bt, hf:hf + 1])
                if bt < 2:
                    nc.vector.tensor_reduce(out=cell_sum[:, bt, hf:hf + 1], in_=row, axis=AX.X, op=ALU.add)
                else:
                    nc.scalar.activation(out=unused_place(), in_=row, func=ACT.Copy, accum_out=cell_sum[:, bt, hf:hf + 1])

            def cell_scalars(bt, stage):
                one = slice(bt, bt + 1)
                if stage == 0:
                    nc.vector.tensor_scalar(out=cell_mean[:, one], in0=cell_sum[:, bt, 0:1], scalar1=cell_sum[:, bt, 1:2],
                                            scalar2=1.0 / H, op0=ALU.add, op1=ALU.mult)
                    nc.vector.scalar_tensor_tensor(out=cell_msq[:, one], in0=cell_sq[:, bt, 0:1], scalar=EPS,
                                                   in1=cell_sq[:, bt, 1:2], op0=ALU.add, op1=ALU.add)
                if stage == 1:
                    nc.vector.scalar_tensor_tensor(out=cell_var[:, one], in0=cell_mean[:, one], scalar=cell_mean[:, one],
                                                   in1=cell_msq[:, one], op0=ALU.mult, op1=ALU.subtract)
                if stage == 2:
                    nc.vector.tensor_scalar(out=cell_var[:, one], in0=cell_var[:, one], scalar1=-1.0, scalar2=EPS,
                                            op0=ALU.mult, op1=ALU.max)
                    nc.gpsimd.tensor_tensor(out=cell_rstd[:, one], in0=cell_var[:, one], in1=neg_half[:, one], op=ALU.pow)

            def centre_and_gain(bt, hf):
                cols = slice(hf * CH, (hf + 1) * CH)
                nc.vector.scalar_tensor_tensor(out=cy_of(bt)[:, cols], in0=flat(cell_rows[(bt, hf)]),
                                               scalar=cell_mean[:, bt:bt + 1], in1=ln_c_w_rows[:, cols],
                                               op0=ALU.subtract, op1=ALU.mult)

            def finish_cy(bt):
                nc.vector.scalar_tensor_tensor(out=cy_of(bt), in0=cy_of(bt), scalar=cell_rstd[:, bt:bt + 1],
                                               in1=ln_c_b_rows[:], op0=ALU.mult, op1=ALU.add)
                nc.sync.dma_start(out=out_1[bt * P:(bt + 1) * P, :], in_=cy_of(bt))
                nc.scalar.activation(out=hy_of(bt), in_=cy_of(bt), func=ACT.Tanh)

            def finish_hy(bt, hf):
                cols = slice(hf * CH, (hf + 1) * CH)
                nc.vector.tensor_tensor(out=hy_of(bt)[:, cols], in0=hy_of(bt)[:, cols], in1=flat(out_rows[(bt, hf)]),
                                        op=ALU.mult)
                nc.sync.dma_start(out=out_0[bt * P:(bt + 1) * P, cols], in_=hy_of(bt)[:, cols])

            def activate_out(k):
                g = outT[:, 2 * k:2 * k + 2, :].rearrange("p h b -> p (h b)")
                nc.scalar.activation(out=g, in_=g, func=ACT.Sigmoid)

            def cell_norm(bt):
                cell_scalars(bt, 0)
                centre_and_gain(bt, 0)
                cell_scalars(bt, 1)
                centre_and_gain(bt, 1)
                cell_scalars(bt, 2)

            banks = [ps_a] * 4 + [ps_b] * 2 + [ps_c] * 2
            for bt in range(NBT):
                for hf in range(2):
                    rows_to_partitions(bt, hf, cellT, banks[2 * bt + hf], cell_rows)
                    cell_sums(bt, hf)
            cell_norm(0)
            cell_norm(1)
            finish_cy(0)
            activate_out(0)
            activate_out(1)
            cell_norm(2)
            finish_cy(1)
            activate_out(2)
            activate_out(3)
            cell_norm(3)
            finish_cy(2)
            finish_cy(3)
            for bt in range(NBT):
                for hf in range(2):
                    rows_to_partitions(bt, hf, outT, banks[2 * bt + hf], out_rows)
                    finish_hy(bt, hf)
